import numpy as np
import ml_dtypes


def mxq(x, axis, fmt="e4m3"):
    dtype, down = {"e4m3": (ml_dtypes.float8_e4m3fn, 7), "e5m2": (ml_dtypes.float8_e5m2, 14)}[fmt]
    v = np.moveaxis(np.asarray(x, np.float32).astype(ml_dtypes.bfloat16).astype(np.float64), axis, -1)
    blocks = v.reshape(v.shape[:-1] + (-1, 32))
    amax = np.abs(blocks).max(-1, keepdims=True)
    byte = np.maximum(np.where(amax > 0, np.frexp(amax)[1] - 1 + 127, 0) - down, 1)
    scale = np.exp2(byte - 127.0)
    codes = (blocks / scale).astype(np.float32).astype(dtype).astype(np.float64)
    return np.moveaxis((codes * scale).reshape(v.shape), -1, axis)


WIDE = False


def mx_kscale(k):
    if not WIDE:
        return np.ones(k)
    levels = np.array([20, -20, 10, -10, 0])
    a = np.random.permutation(np.resize(levels, k // 512 * 4)).reshape(k // 512, 4)
    idx = np.arange(k)
    return np.exp2(a[idx // 512, idx % 128 // 32])


BF16 = ml_dtypes.bfloat16


def bf(x):
    return np.asarray(x, np.float32).astype(BF16)


def f64(x):
    return np.asarray(x).astype(np.float64)


B, I, H = 4096, 512, 512
K = I + H
EPS = 1e-6


def setup_inputs():
    u = mx_kscale(H)
    x = bf(np.random.standard_normal((B, I)))
    h = bf(np.random.standard_normal((B, H)))
    time_delta = bf(np.random.uniform(0.0, 1.0, (B, 1)))
    W_mod0 = bf(np.random.standard_normal((K, H)) * 0.6 / np.sqrt(K))
    b_mod = bf(np.random.standard_normal(H) * 0.2)
    W_tgt0 = bf(np.random.standard_normal((K, H)) * 0.6 / np.sqrt(K))
    b_tgt = bf(np.random.standard_normal(H) * 0.2)
    log_tau = bf(np.random.standard_normal(H) * 0.2)
    bias = bf(np.random.standard_normal(H) * 0.1)
    g = bf(np.random.standard_normal((B, H)) * np.exp2(np.random.randint(-12, 1, (B, 1))) * 64.0 * u)
    c = np.concatenate([f64(x), f64(h)], axis=-1)
    f = np.tanh(c @ f64(W_mod0) + f64(b_mod))
    a = np.tanh(c @ f64(W_tgt0) + f64(b_tgt))
    return {"x": x, "h": h, "time_delta": time_delta,
            "W_mod": bf(f64(W_mod0) / u[None, :]), "b_mod": b_mod,
            "W_tgt": bf(f64(W_tgt0) / u[None, :]), "b_tgt": b_tgt,
            "log_tau": log_tau, "bias": bias,
            "f": np.asarray(f, np.float32), "a": np.asarray(a, np.float32),
            "grad_out": g}


def reference(x, h, time_delta, W_mod, b_mod, W_tgt, b_tgt, log_tau, bias, f, a, grad_out):
    g = f64(grad_out)
    hf = f64(h)
    ff = f64(f)
    af = f64(a)
    td = f64(time_delta)
    tau = np.exp(f64(log_tau))[None, :]
    tau_sys = tau / (1.0 + tau * np.abs(ff))
    q = tau_sys + EPS
    decay = np.exp(-td / q)
    da = g * (1.0 - decay) * (1.0 - af * af)
    df = -g * (hf - af - f64(bias)) * decay * td * (tau_sys / q) ** 2 * np.sign(ff) * (1.0 - ff * ff)
    wm = f64(W_mod)[:I]
    wt = f64(W_tgt)[:I]
    p_mod = mxq(df, 1, "e5m2") @ mxq(wm, 1, "e4m3").T
    p_tgt = mxq(da, 1, "e5m2") @ mxq(wt, 1, "e4m3").T
    return p_mod + p_tgt

@@ -1,0 +1,290 @@
+import math
+from contextlib import ExitStack
+
+import concourse.mybir as mybir
+from concourse.masks import make_identity
+
+F32 = mybir.dt.float32
+BF16 = mybir.dt.bfloat16
+I32 = mybir.dt.int32
+U32 = mybir.dt.uint32
+U8 = mybir.dt.uint8
+E4M3_X4 = mybir.dt.float8_e4m3fn_x4
+E5M2_X4 = mybir.dt.float8_e5m2_x4
+ACT = mybir.ActivationFunctionType
+ALU = mybir.AluOpType
+
+P = 128
+TOKENS, HIDDEN, OUT_FEATURES = 4096, 512, 512
+EPS = 1e-6
+TILES = TOKENS // P
+PACK = HIDDEN // P
+BLOCK = 4
+GROUP = 8
+CHAIN_OPS = 4
+PREP_AHEAD = 2 * GROUP - 1
+LOAD_AHEAD = 2
+
+FLOPS = 2 * TOKENS * OUT_FEATURES * 2 * HIDDEN
+BYTES = TOKENS * HIDDEN * (2 + 2 + 4 + 4) + TOKENS * OUT_FEATURES * 4 + 2 * OUT_FEATURES * HIDDEN * 2
+
+BY_WORD = "p j t -> p t j"
+
+
+def tile_ltccell_t_v_kernel(
+    tc, x, h, time_delta, W_mod, b_mod, W_tgt, b_tgt, log_tau, bias, f, a, grad_out, out
+):
+    nc = tc.nc
+    by_tile = "(p t) k -> p t k"
+    f_rows = f.rearrange(by_tile, t=TILES)
+    a_rows = a.rearrange(by_tile, t=TILES)
+    h_rows = h.rearrange(by_tile, t=TILES)
+    g_rows = grad_out.rearrange(by_tile, t=TILES)
+    out_rows = out.rearrange(by_tile, t=TILES)
+
+    with ExitStack() as stack:
+        stack.enter_context(tc.manual_schedule())
+        const = stack.enter_context(tc.tile_pool(name="const", bufs=1))
+        setup = stack.enter_context(tc.tile_pool(name="setup", bufs=2))
+        work = stack.enter_context(tc.tile_pool(name="work", bufs=2))
+        psum = stack.enter_context(tc.psum_pool(name="psum", bufs=1))
+
+        ident_f32 = const.tile([P, P], F32, name="ident_f32")
+        make_identity(nc, ident_f32[:])
+        ident_bf16 = const.tile([P, P], BF16, name="ident_bf16")
+        make_identity(nc, ident_bf16[:])
+
+        log_tau_rows = const.tile([P, HIDDEN], BF16, name="log_tau_rows")
+        nc.scalar.dma_start(out=log_tau_rows[:], in_=log_tau.partition_broadcast(P))
+        delta = const.tile([P, TILES], BF16, name="delta")
+        nc.scalar.dma_start(out=delta[:], in_=time_delta.rearrange("(p t) o -> p (t o)", t=TILES))
+        bias_bf16 = const.tile([P, HIDDEN], BF16, name="bias_bf16")
+        nc.scalar.dma_start(out=bias_bf16[:], in_=bias.partition_broadcast(P))
+
+        inv_tau = const.tile([P, HIDDEN], F32, name="inv_tau")
+        nc.scalar.activation(out=inv_tau[:], in_=log_tau_rows[:], func=ACT.Exp, scale=-1.0)
+        bias_rows = const.tile([P, HIDDEN], F32, name="bias_rows")
+        nc.vector.tensor_copy(out=bias_rows[:], in_=bias_bf16[:])
+        minus_delta = const.tile([P, TILES], F32, name="minus_delta")
+        nc.vector.tensor_scalar(out=minus_delta[:], in0=delta[:], scalar1=-1.0, scalar2=None, op0=ALU.mult)
+        minus_delta_over_eps = const.tile([P, TILES], F32, name="minus_delta_over_eps")
+        nc.vector.tensor_scalar(
+            out=minus_delta_over_eps[:], in0=delta[:], scalar1=-1.0 / EPS, scalar2=None, op0=ALU.mult
+        )
+
+        def load_weight(w):
+            raw = setup.tile([P, PACK, HIDDEN], BF16, name="w_raw", tag="w_raw")
+            nc.scalar.dma_start(out=raw[:], in_=w[0:OUT_FEATURES, :].rearrange("(c p) k -> p c k", p=P))
+            return raw
+
+        def quantise_weight(raw, label):
+            grouped = setup.tile([P, OUT_FEATURES, PACK], BF16, name="w_grouped", tag="w_grouped", align_bytes=64)
+            for c in range(OUT_FEATURES // P):
+                flipped = psum.tile([P, PACK, P], BF16, name="w_flipped", tag="gT")
+                for j in range(PACK):
+                    nc.tensor.transpose(flipped[:, j, :], raw[:, c, j * P : (j + 1) * P], ident_bf16[:])
+                nc.vector.tensor_copy(out=grouped[:, c * P : (c + 1) * P, :], in_=flipped[:].rearrange(BY_WORD))
+            codes = const.tile([P, OUT_FEATURES], U32, name="codes_" + label, align_bytes=64)
+            scales = const.tile([P, OUT_FEATURES], U8, name="scales_" + label, align_bytes=64)
+            nc.vector.quantize_mx(
+                out=codes[:].bitcast(E4M3_X4), scales=scales[:], in_=grouped[:].rearrange("p i j -> p (i j)")
+            )
+            return codes, scales
+
+        raw_mod = load_weight(W_mod)
+        raw_tgt = load_weight(W_tgt)
+
+        s_tile, decay, sign_f = {}, {}, {}
+        f_blk, a_blk, h_blk, g_blk, out_blk = {}, {}, {}, {}, {}
+        f_sq, a_sq, minus_h, g_signed, x7 = {}, {}, {}, {}, {}
+        gT, eT, mT, xT = {}, {}, {}, {}
+        grads, grad_codes, grad_scales = {}, {}, {}
+
+        def row(blocks, t):
+            return blocks[t // BLOCK][:, t % BLOCK, :]
+
+        def flip(dst, src, ident):
+            for j in range(PACK):
+                nc.tensor.transpose(dst[:, j, :], src[:, j * P : (j + 1) * P], ident[:])
+
+        def load_f_for_d(t):
+            s_tile[t] = work.tile([P, HIDDEN], F32, name="s_tile", tag="s_tile", bufs=PREP_AHEAD + LOAD_AHEAD + 2)
+            nc.sync.dma_start(out=s_tile[t][:], in_=f_rows[:, t, :])
+
+        def load_block(b):
+            tiles = slice(b * BLOCK, (b + 1) * BLOCK)
+            f_blk[b] = work.tile([P, BLOCK, HIDDEN], F32, name="f_blk", tag="f_blk", bufs=3)
+            nc.sync.dma_start(out=f_blk[b][:], in_=f_rows[:, tiles, :])
+            a_blk[b] = work.tile([P, BLOCK, HIDDEN], F32, name="a_blk", tag="a_blk", bufs=3)
+            nc.sync.dma_start(out=a_blk[b][:], in_=a_rows[:, tiles, :])
+            h_blk[b] = work.tile([P, BLOCK, HIDDEN], BF16, name="h_blk", tag="h_blk", bufs=3)
+            nc.sync.dma_start(out=h_blk[b][:], in_=h_rows[:, tiles, :])
+            g_blk[b] = work.tile([P, BLOCK, HIDDEN], BF16, name="g_blk", tag="g_blk", bufs=3)
+            nc.sync.dma_start(out=g_blk[b][:], in_=g_rows[:, tiles, :])
+
+        def clear_sign(t):
+            words = s_tile[t][:].bitcast(I32)
+            nc.vector.tensor_scalar(out=words, in0=words, scalar1=0x7FFFFFFF, scalar2=None, op0=ALU.bitwise_and)
+
+        def add_inv_tau(t):
+            nc.vector.tensor_tensor(out=s_tile[t][:], in0=s_tile[t][:], in1=inv_tau[:], op=ALU.add)
+
+        def chain_op(group, n):
+            first = group * GROUP
+            if n < GROUP:
+                t = first + n
+                nc.scalar.activation(out=s_tile[t][:], in_=s_tile[t][:], func=ACT.Ln)
+            elif n < 2 * GROUP:
+                t = first + n - GROUP
+                nc.scalar.activation(out=s_tile[t][:], in_=s_tile[t][:], func=ACT.Sigmoid, bias=math.log(EPS))
+            elif n % 2 == 0:
+                t = first + (n - 2 * GROUP) // 2
+                decay[t] = work.tile([P, HIDDEN], F32, name="decay", tag="decay", bufs=GROUP + 2)
+                nc.scalar.activation(
+                    out=decay[t][:], in_=s_tile[t][:], func=ACT.Exp, scale=minus_delta_over_eps[:, t : t + 1]
+                )
+            else:
+                t = first + (n - 2 * GROUP) // 2
+                nc.scalar.activation(out=s_tile[t][:], in_=s_tile[t][:], func=ACT.Square, scale=-1.0, bias=1.0)
+
+        def squares_and_sign(t):
+            sign_f[t] = work.tile([P, HIDDEN], BF16, name="sign_f", tag="sign_f", bufs=3)
+            nc.scalar.activation(out=sign_f[t][:], in_=row(f_blk, t), func=ACT.Sign)
+            fT = psum.tile([P, PACK, P], F32, name="fT", tag="fT")
+            flip(fT, row(f_blk, t), ident_f32)
+            aT = psum.tile([P, PACK, P], F32, name="aT", tag="aT")
+            flip(aT, row(a_blk, t), ident_f32)
+            f_sq[t] = work.tile([P, P, PACK], F32, name="f_sq", tag="f_sq", bufs=3)
+            nc.scalar.activation(out=f_sq[t][:], in_=fT[:].rearrange(BY_WORD), func=ACT.Square)
+            a_sq[t] = work.tile([P, P, PACK], F32, name="a_sq", tag="a_sq", bufs=3)
+            nc.scalar.activation(out=a_sq[t][:], in_=aT[:].rearrange(BY_WORD), func=ACT.Square)
+
+        def finish_gradients(t):
+            u = work.tile([P, P, PACK], F32, name="u", tag="u")
+            nc.vector.scalar_tensor_tensor(
+                out=u[:], in0=a_sq[t][:], scalar=1.0, in1=gT[t][:].rearrange(BY_WORD), op0=ALU.subtract, op1=ALU.mult
+            )
+            x8 = work.tile([P, P, PACK], F32, name="x8", tag="x8")
+            nc.vector.scalar_tensor_tensor(
+                out=x8[:], in0=f_sq[t][:], scalar=1.0, in1=xT[t][:].rearrange(BY_WORD), op0=ALU.subtract, op1=ALU.mult
+            )
+            grads[t] = work.tile([P, 2, P, PACK], BF16, name="grads", tag="grads", align_bytes=64)
+            nc.vector.scalar_tensor_tensor(
+                out=grads[t][:, 1, :, :], in0=eT[t][:].rearrange(BY_WORD), scalar=1.0, in1=u[:],
+                op0=ALU.subtract, op1=ALU.mult,
+            )
+            nc.vector.tensor_tensor(out=grads[t][:, 0, :, :], in0=mT[t][:].rearrange(BY_WORD), in1=x8[:], op=ALU.mult)
+
+        def quantise_gradients(t):
+            grad_codes[t] = work.tile([P, 2 * P], U32, name="grad_codes", tag="grad_codes", align_bytes=64)
+            grad_scales[t] = work.tile([P, 2 * P], U8, name="grad_scales", tag="grad_scales", align_bytes=64)
+            nc.vector.quantize_mx(
+                out=grad_codes[t][:].bitcast(E5M2_X4),
+                scales=grad_scales[t][:],
+                in_=grads[t][:].rearrange("p s t j -> p (s t j)"),
+            )
+
+        def decay_times_ratio(t):
+            x5 = work.tile([P, HIDDEN], F32, name="x5", tag="x5")
+            nc.vector.tensor_tensor(out=x5[:], in0=decay[t][:], in1=s_tile[t][:], op=ALU.mult)
+            return x5
+
+        def sign_the_gradient(t):
+            g_signed[t] = work.tile([P, HIDDEN], BF16, name="g_signed", tag="g_signed")
+            nc.vector.tensor_tensor(out=g_signed[t][:], in0=row(g_blk, t), in1=sign_f[t][:], op=ALU.mult)
+
+        def times_delta_and_gradient(t, x5):
+            x7[t] = work.tile([P, HIDDEN], F32, name="x7", tag="x7")
+            nc.vector.scalar_tensor_tensor(
+                out=x7[t][:], in0=x5[:], scalar=minus_delta[:, t : t + 1], in1=g_signed[t][:],
+                op0=ALU.mult, op1=ALU.mult,
+            )
+
+        def negate_h(t):
+            minus_h[t] = work.tile([P, HIDDEN], F32, name="minus_h", tag="minus_h")
+            nc.vector.tensor_scalar(out=minus_h[t][:], in0=row(h_blk, t), scalar1=-1.0, scalar2=None, op0=ALU.mult)
+
+        def flip_inputs_of_the_products(t):
+            gT[t] = psum.tile([P, PACK, P], BF16, name="gT", tag="gT")
+            flip(gT[t], row(g_blk, t), ident_bf16)
+            eT[t] = psum.tile([P, PACK, P], F32, name="eT", tag="eT")
+            flip(eT[t], decay[t], ident_f32)
+            mT[t] = psum.tile([P, PACK, P], F32, name="mT", tag="mT")
+            terms = (row(a_blk, t), minus_h[t], bias_rows)
+            for j in range(PACK):
+                for n, term in enumerate(terms):
+                    nc.tensor.matmul(
+                        out=mT[t][:, j, :], lhsT=term[:, j * P : (j + 1) * P], rhs=ident_f32[:], is_transpose=True,
+                        start=(n == 0), stop=(n == len(terms) - 1),
+                    )
+
+        def flip_x7(t):
+            xT[t] = psum.tile([P, PACK, P], F32, name="xT", tag="xT")
+            flip(xT[t], x7[t], ident_f32)
+
+        def multiply(t):
+            acc = psum.tile([P, OUT_FEATURES], F32, name="acc", tag="acc", bufs=2)
+            for n, (codes, scales) in enumerate((weight_mod, weight_tgt)):
+                tokens = slice(n * P, (n + 1) * P)
+                nc.tensor.matmul_mx(
+                    out=acc[:],
+                    lhsT=grad_codes[t][:, tokens].bitcast(E5M2_X4),
+                    lhsT_scale=grad_scales[t][:, tokens],
+                    rhs=codes[:].bitcast(E4M3_X4),
+                    rhs_scale=scales[:],
+                    start=(n == 0),
+                    stop=(n == 1),
+                )
+            return acc
+
+        def store(t, acc):
+            b = t // BLOCK
+            if t % BLOCK == 0:
+                out_blk[b] = work.tile([P, BLOCK, OUT_FEATURES], F32, name="out_blk", tag="out_blk")
+            nc.scalar.copy(out=row(out_blk, t), in_=acc[:])
+            if t % BLOCK == BLOCK - 1:
+                nc.sync.dma_start(out=out_rows[:, b * BLOCK : (b + 1) * BLOCK, :], in_=out_blk[b][:])
+
+        def is_tile(t):
+            return 0 <= t < TILES
+
+        def step(s):
+            if is_tile(s + PREP_AHEAD + LOAD_AHEAD):
+                load_f_for_d(s + PREP_AHEAD + LOAD_AHEAD)
+            if (s + 1 + BLOCK) % BLOCK == 0 and is_tile(s + 1 + BLOCK):
+                load_block((s + 1 + BLOCK) // BLOCK)
+            if is_tile(s + 1):
+                squares_and_sign(s + 1)
+            if is_tile((s // GROUP + 1) * GROUP):
+                for n in range(CHAIN_OPS * (s % GROUP), CHAIN_OPS * (s % GROUP + 1)):
+                    chain_op(s // GROUP + 1, n)
+            if is_tile(s - 1):
+                finish_gradients(s - 1)
+            if is_tile(s):
+                x5 = decay_times_ratio(s)
+                sign_the_gradient(s)
+            if is_tile(s + PREP_AHEAD):
+                clear_sign(s + PREP_AHEAD)
+            if is_tile(s - 1):
+                quantise_gradients(s - 1)
+            if is_tile(s):
+                times_delta_and_gradient(s, x5)
+            if is_tile(s + 1):
+                negate_h(s + 1)
+            if is_tile(s + PREP_AHEAD):
+                add_inv_tau(s + PREP_AHEAD)
+            if is_tile(s):
+                flip_inputs_of_the_products(s)
+            if is_tile(s - 1):
+                acc = multiply(s - 1)
+            if is_tile(s):
+                flip_x7(s)
+            if is_tile(s - 1):
+                store(s - 1, acc)
+
+        for s in range(-(PREP_AHEAD + LOAD_AHEAD), 0):
+            step(s)
+        weight_mod = quantise_weight(raw_mod, "mod")
+        weight_tgt = quantise_weight(raw_tgt, "tgt")
+        for s in range(0, TILES + 1):
+            step(s)

@@ -58,13 +58,11 @@ def tile_ltccell_t_v_kernel(
         nc.scalar.dma_start(out=log_tau_rows[:], in_=log_tau.partition_broadcast(P))
         delta = const.tile([P, TILES], BF16, name="delta")
         nc.scalar.dma_start(out=delta[:], in_=time_delta.rearrange("(p t) o -> p (t o)", t=TILES))
-        bias_bf16 = const.tile([P, HIDDEN], BF16, name="bias_bf16")
-        nc.scalar.dma_start(out=bias_bf16[:], in_=bias.partition_broadcast(P))
+        bias_rows = const.tile([P, HIDDEN], BF16, name="bias_rows")
+        nc.scalar.dma_start(out=bias_rows[:], in_=bias.partition_broadcast(P))
 
         inv_tau = const.tile([P, HIDDEN], F32, name="inv_tau")
         nc.scalar.activation(out=inv_tau[:], in_=log_tau_rows[:], func=ACT.Exp, scale=-1.0)
-        bias_rows = const.tile([P, HIDDEN], F32, name="bias_rows")
-        nc.vector.tensor_copy(out=bias_rows[:], in_=bias_bf16[:])
         minus_delta = const.tile([P, TILES], F32, name="minus_delta")
         nc.vector.tensor_scalar(out=minus_delta[:], in0=delta[:], scalar1=-1.0, scalar2=None, op0=ALU.mult)
         minus_delta_over_eps = const.tile([P, TILES], F32, name="minus_delta_over_eps")
@@ -96,7 +94,7 @@ def tile_ltccell_t_v_kernel(
 
         s_tile, decay, sign_f = {}, {}, {}
         f_blk, a_blk, h_blk, g_blk, out_blk = {}, {}, {}, {}, {}
-        f_sq, a_sq, minus_h, g_signed, x7 = {}, {}, {}, {}, {}
+        f_sq, a_sq, m_rows, g_signed, x7 = {}, {}, {}, {}, {}
         gT, eT, mT, xT = {}, {}, {}, {}
         grads, grad_codes, grad_scales = {}, {}, {}
 
@@ -200,9 +198,10 @@ def tile_ltccell_t_v_kernel(
                 op0=ALU.mult, op1=ALU.mult,
             )
 
-        def negate_h(t):
-            minus_h[t] = work.tile([P, HIDDEN], F32, name="minus_h", tag="minus_h")
-            nc.vector.tensor_scalar(out=minus_h[t][:], in0=row(h_blk, t), scalar1=-1.0, scalar2=None, op0=ALU.mult)
+        def a_minus_h_plus_bias(t):
+            m_rows[t] = work.tile([P, HIDDEN], F32, name="m_rows", tag="m_rows")
+            nc.gpsimd.tensor_tensor(out=m_rows[t][:], in0=row(a_blk, t), in1=row(h_blk, t), op=ALU.subtract)
+            nc.gpsimd.tensor_tensor(out=m_rows[t][:], in0=m_rows[t][:], in1=bias_rows[:], op=ALU.add)
 
         def flip_inputs_of_the_products(t):
             gT[t] = psum.tile([P, PACK, P], BF16, name="gT", tag="gT")
@@ -210,13 +209,7 @@ def tile_ltccell_t_v_kernel(
             eT[t] = psum.tile([P, PACK, P], F32, name="eT", tag="eT")
             flip(eT[t], decay[t], ident_f32)
             mT[t] = psum.tile([P, PACK, P], F32, name="mT", tag="mT")
-            terms = (row(a_blk, t), minus_h[t], bias_rows)
-            for j in range(PACK):
-                for n, term in enumerate(terms):
-                    nc.tensor.matmul(
-                        out=mT[t][:, j, :], lhsT=term[:, j * P : (j + 1) * P], rhs=ident_f32[:], is_transpose=True,
-                        start=(n == 0), stop=(n == len(terms) - 1),
-                    )
+            flip(mT[t], m_rows[t], ident_f32)
 
         def flip_x7(t):
             xT[t] = psum.tile([P, PACK, P], F32, name="xT", tag="xT")
@@ -270,7 +263,7 @@ def tile_ltccell_t_v_kernel(
             if is_tile(s):
                 times_delta_and_gradient(s, x5)
             if is_tile(s + 1):
-                negate_h(s + 1)
+                a_minus_h_plus_bias(s + 1)
             if is_tile(s + PREP_AHEAD):
                 add_inv_tau(s + PREP_AHEAD)
             if is_tile(s):

@@ -23,7 +23,7 @@ BLOCK = 4
 GROUP = 8
 CHAIN_OPS = 4
 PREP_AHEAD = 2 * GROUP - 1
-LOAD_AHEAD = 2
+LOAD_AHEAD = 4
 
 FLOPS = 2 * TOKENS * OUT_FEATURES * 2 * HIDDEN
 BYTES = TOKENS * HIDDEN * (2 + 2 + 4 + 4) + TOKENS * OUT_FEATURES * 4 + 2 * OUT_FEATURES * HIDDEN * 2
@@ -96,7 +96,7 @@ def tile_ltccell_t_v_kernel(
         f_blk, a_blk, h_blk, g_blk, out_blk = {}, {}, {}, {}, {}
         f_sq, a_sq, m_rows, g_signed, x7 = {}, {}, {}, {}, {}
         gT, eT, mT, xT = {}, {}, {}, {}
-        grads, grad_codes, grad_scales = {}, {}, {}
+        grads, grad_codes, grad_scales, acc = {}, {}, {}, {}
 
         def row(blocks, t):
             return blocks[t // BLOCK][:, t % BLOCK, :]
@@ -203,24 +203,22 @@ def tile_ltccell_t_v_kernel(
             nc.gpsimd.tensor_tensor(out=m_rows[t][:], in0=row(a_blk, t), in1=row(h_blk, t), op=ALU.subtract)
             nc.gpsimd.tensor_tensor(out=m_rows[t][:], in0=m_rows[t][:], in1=bias_rows[:], op=ALU.add)
 
-        def flip_inputs_of_the_products(t):
+        def flip_factors(t):
             gT[t] = psum.tile([P, PACK, P], BF16, name="gT", tag="gT")
             flip(gT[t], row(g_blk, t), ident_bf16)
+            xT[t] = psum.tile([P, PACK, P], F32, name="xT", tag="xT")
+            flip(xT[t], x7[t], ident_f32)
             eT[t] = psum.tile([P, PACK, P], F32, name="eT", tag="eT")
             flip(eT[t], decay[t], ident_f32)
             mT[t] = psum.tile([P, PACK, P], F32, name="mT", tag="mT")
             flip(mT[t], m_rows[t], ident_f32)
 
-        def flip_x7(t):
-            xT[t] = psum.tile([P, PACK, P], F32, name="xT", tag="xT")
-            flip(xT[t], x7[t], ident_f32)
-
         def multiply(t):
-            acc = psum.tile([P, OUT_FEATURES], F32, name="acc", tag="acc", bufs=2)
+            acc[t] = psum.tile([P, OUT_FEATURES], F32, name="acc", tag="acc", bufs=2)
             for n, (codes, scales) in enumerate((weight_mod, weight_tgt)):
                 tokens = slice(n * P, (n + 1) * P)
                 nc.tensor.matmul_mx(
-                    out=acc[:],
+                    out=acc[t][:],
                     lhsT=grad_codes[t][:, tokens].bitcast(E5M2_X4),
                     lhsT_scale=grad_scales[t][:, tokens],
                     rhs=codes[:].bitcast(E4M3_X4),
@@ -228,13 +226,12 @@ def tile_ltccell_t_v_kernel(
                     start=(n == 0),
                     stop=(n == 1),
                 )
-            return acc
 
-        def store(t, acc):
+        def store(t):
             b = t // BLOCK
             if t % BLOCK == 0:
                 out_blk[b] = work.tile([P, BLOCK, OUT_FEATURES], F32, name="out_blk", tag="out_blk")
-            nc.scalar.copy(out=row(out_blk, t), in_=acc[:])
+            nc.scalar.copy(out=row(out_blk, t), in_=acc[t][:])
             if t % BLOCK == BLOCK - 1:
                 nc.sync.dma_start(out=out_rows[:, b * BLOCK : (b + 1) * BLOCK, :], in_=out_blk[b][:])
 
@@ -251,33 +248,31 @@ def tile_ltccell_t_v_kernel(
             if is_tile((s // GROUP + 1) * GROUP):
                 for n in range(CHAIN_OPS * (s % GROUP), CHAIN_OPS * (s % GROUP + 1)):
                     chain_op(s // GROUP + 1, n)
-            if is_tile(s - 1):
-                finish_gradients(s - 1)
             if is_tile(s):
                 x5 = decay_times_ratio(s)
                 sign_the_gradient(s)
             if is_tile(s + PREP_AHEAD):
                 clear_sign(s + PREP_AHEAD)
-            if is_tile(s - 1):
-                quantise_gradients(s - 1)
             if is_tile(s):
                 times_delta_and_gradient(s, x5)
             if is_tile(s + 1):
                 a_minus_h_plus_bias(s + 1)
+            if is_tile(s - 1):
+                finish_gradients(s - 1)
             if is_tile(s + PREP_AHEAD):
                 add_inv_tau(s + PREP_AHEAD)
-            if is_tile(s):
-                flip_inputs_of_the_products(s)
             if is_tile(s - 1):
-                acc = multiply(s - 1)
+                quantise_gradients(s - 1)
             if is_tile(s):
-                flip_x7(s)
+                flip_factors(s)
             if is_tile(s - 1):
-                store(s - 1, acc)
+                multiply(s - 1)
+            if is_tile(s - 2):
+                store(s - 2)
 
         for s in range(-(PREP_AHEAD + LOAD_AHEAD), 0):
             step(s)
         weight_mod = quantise_weight(raw_mod, "mod")
         weight_tgt = quantise_weight(raw_tgt, "tgt")
-        for s in range(0, TILES + 1):
+        for s in range(0, TILES + 2):
             step(s)

@@ -94,8 +94,8 @@ def tile_ltccell_t_v_kernel(
 
         s_tile, decay, sign_f = {}, {}, {}
         f_blk, a_blk, h_blk, g_blk, out_blk = {}, {}, {}, {}, {}
-        f_sq, a_sq, m_rows, g_signed, x7 = {}, {}, {}, {}, {}
-        gT, eT, mT, xT = {}, {}, {}, {}
+        f_sq, a_sq, m_rows, g_signed, x9, u = {}, {}, {}, {}, {}, {}
+        gT, eT, xT = {}, {}, {}
         grads, grad_codes, grad_scales, acc = {}, {}, {}, {}
 
         def row(blocks, t):
@@ -157,21 +157,22 @@ def tile_ltccell_t_v_kernel(
             a_sq[t] = work.tile([P, P, PACK], F32, name="a_sq", tag="a_sq", bufs=3)
             nc.scalar.activation(out=a_sq[t][:], in_=aT[:].rearrange(BY_WORD), func=ACT.Square)
 
-        def finish_gradients(t):
-            u = work.tile([P, P, PACK], F32, name="u", tag="u")
+        def gradient_times_a_factor(t):
+            u[t] = work.tile([P, P, PACK], F32, name="u", tag="u")
             nc.vector.scalar_tensor_tensor(
-                out=u[:], in0=a_sq[t][:], scalar=1.0, in1=gT[t][:].rearrange(BY_WORD), op0=ALU.subtract, op1=ALU.mult
+                out=u[t][:], in0=a_sq[t][:], scalar=1.0, in1=gT[t][:].rearrange(BY_WORD), op0=ALU.subtract, op1=ALU.mult
             )
-            x8 = work.tile([P, P, PACK], F32, name="x8", tag="x8")
-            nc.vector.scalar_tensor_tensor(
-                out=x8[:], in0=f_sq[t][:], scalar=1.0, in1=xT[t][:].rearrange(BY_WORD), op0=ALU.subtract, op1=ALU.mult
-            )
+
+        def finish_da_and_df(t):
             grads[t] = work.tile([P, 2, P, PACK], BF16, name="grads", tag="grads", align_bytes=64)
             nc.vector.scalar_tensor_tensor(
-                out=grads[t][:, 1, :, :], in0=eT[t][:].rearrange(BY_WORD), scalar=1.0, in1=u[:],
+                out=grads[t][:, 1, :, :], in0=eT[t][:].rearrange(BY_WORD), scalar=1.0, in1=u[t][:],
                 op0=ALU.subtract, op1=ALU.mult,
             )
-            nc.vector.tensor_tensor(out=grads[t][:, 0, :, :], in0=mT[t][:].rearrange(BY_WORD), in1=x8[:], op=ALU.mult)
+            nc.vector.scalar_tensor_tensor(
+                out=grads[t][:, 0, :, :], in0=f_sq[t][:], scalar=1.0, in1=xT[t][:].rearrange(BY_WORD),
+                op0=ALU.subtract, op1=ALU.mult,
+            )
 
         def quantise_gradients(t):
             grad_codes[t] = work.tile([P, 2 * P], U32, name="grad_codes", tag="grad_codes", align_bytes=64)
@@ -192,11 +193,16 @@ def tile_ltccell_t_v_kernel(
             nc.vector.tensor_tensor(out=g_signed[t][:], in0=row(g_blk, t), in1=sign_f[t][:], op=ALU.mult)
 
         def times_delta_and_gradient(t, x5):
-            x7[t] = work.tile([P, HIDDEN], F32, name="x7", tag="x7")
+            x7 = work.tile([P, HIDDEN], F32, name="x7", tag="x7")
             nc.vector.scalar_tensor_tensor(
-                out=x7[t][:], in0=x5[:], scalar=minus_delta[:, t : t + 1], in1=g_signed[t][:],
+                out=x7[:], in0=x5[:], scalar=minus_delta[:, t : t + 1], in1=g_signed[t][:],
                 op0=ALU.mult, op1=ALU.mult,
             )
+            return x7
+
+        def times_state_difference(t, x7):
+            x9[t] = work.tile([P, HIDDEN], F32, name="x9", tag="x9")
+            nc.vector.tensor_tensor(out=x9[t][:], in0=x7[:], in1=m_rows[t][:], op=ALU.mult)
 
         def a_minus_h_plus_bias(t):
             m_rows[t] = work.tile([P, HIDDEN], F32, name="m_rows", tag="m_rows")
@@ -206,12 +212,10 @@ def tile_ltccell_t_v_kernel(
         def flip_factors(t):
             gT[t] = psum.tile([P, PACK, P], BF16, name="gT", tag="gT")
             flip(gT[t], row(g_blk, t), ident_bf16)
-            xT[t] = psum.tile([P, PACK, P], F32, name="xT", tag="xT")
-            flip(xT[t], x7[t], ident_f32)
             eT[t] = psum.tile([P, PACK, P], F32, name="eT", tag="eT")
             flip(eT[t], decay[t], ident_f32)
-            mT[t] = psum.tile([P, PACK, P], F32, name="mT", tag="mT")
-            flip(mT[t], m_rows[t], ident_f32)
+            xT[t] = psum.tile([P, PACK, P], F32, name="xT", tag="xT")
+            flip(xT[t], x9[t], ident_f32)
 
         def multiply(t):
             acc[t] = psum.tile([P, OUT_FEATURES], F32, name="acc", tag="acc", bufs=2)
@@ -249,16 +253,20 @@ def tile_ltccell_t_v_kernel(
                 for n in range(CHAIN_OPS * (s % GROUP), CHAIN_OPS * (s % GROUP + 1)):
                     chain_op(s // GROUP + 1, n)
             if is_tile(s):
-                x5 = decay_times_ratio(s)
                 sign_the_gradient(s)
+                x5 = decay_times_ratio(s)
             if is_tile(s + PREP_AHEAD):
                 clear_sign(s + PREP_AHEAD)
             if is_tile(s):
-                times_delta_and_gradient(s, x5)
+                x7 = times_delta_and_gradient(s, x5)
             if is_tile(s + 1):
                 a_minus_h_plus_bias(s + 1)
             if is_tile(s - 1):
-                finish_gradients(s - 1)
+                gradient_times_a_factor(s - 1)
+            if is_tile(s):
+                times_state_difference(s, x7)
+            if is_tile(s - 1):
+                finish_da_and_df(s - 1)
             if is_tile(s + PREP_AHEAD):
                 add_inv_tau(s + PREP_AHEAD)
             if is_tile(s - 1):

@@ -58,11 +58,13 @@ def tile_ltccell_t_v_kernel(
         nc.scalar.dma_start(out=log_tau_rows[:], in_=log_tau.partition_broadcast(P))
         delta = const.tile([P, TILES], BF16, name="delta")
         nc.scalar.dma_start(out=delta[:], in_=time_delta.rearrange("(p t) o -> p (t o)", t=TILES))
-        bias_rows = const.tile([P, HIDDEN], BF16, name="bias_rows")
-        nc.scalar.dma_start(out=bias_rows[:], in_=bias.partition_broadcast(P))
+        bias_bf16 = const.tile([P, HIDDEN], BF16, name="bias_bf16")
+        nc.scalar.dma_start(out=bias_bf16[:], in_=bias.partition_broadcast(P))
 
         inv_tau = const.tile([P, HIDDEN], F32, name="inv_tau")
         nc.scalar.activation(out=inv_tau[:], in_=log_tau_rows[:], func=ACT.Exp, scale=-1.0)
+        bias_rows = const.tile([P, HIDDEN], F32, name="bias_rows")
+        nc.vector.tensor_copy(out=bias_rows[:], in_=bias_bf16[:])
         minus_delta = const.tile([P, TILES], F32, name="minus_delta")
         nc.vector.tensor_scalar(out=minus_delta[:], in0=delta[:], scalar1=-1.0, scalar2=None, op0=ALU.mult)
         minus_delta_over_eps = const.tile([P, TILES], F32, name="minus_delta_over_eps")
@@ -94,8 +96,8 @@ def tile_ltccell_t_v_kernel(
 
         s_tile, decay, sign_f = {}, {}, {}
         f_blk, a_blk, h_blk, g_blk, out_blk = {}, {}, {}, {}, {}
-        f_sq, a_sq, m_rows, g_signed, x9, u = {}, {}, {}, {}, {}, {}
-        gT, eT, xT = {}, {}, {}
+        f_sq, a_sq, minus_h, g_signed, x7 = {}, {}, {}, {}, {}
+        gT, eT, mT, xT = {}, {}, {}, {}
         grads, grad_codes, grad_scales, acc = {}, {}, {}, {}
 
         def row(blocks, t):
@@ -157,22 +159,21 @@ def tile_ltccell_t_v_kernel(
             a_sq[t] = work.tile([P, P, PACK], F32, name="a_sq", tag="a_sq", bufs=3)
             nc.scalar.activation(out=a_sq[t][:], in_=aT[:].rearrange(BY_WORD), func=ACT.Square)
 
-        def gradient_times_a_factor(t):
-            u[t] = work.tile([P, P, PACK], F32, name="u", tag="u")
+        def finish_gradients(t):
+            u = work.tile([P, P, PACK], F32, name="u", tag="u")
             nc.vector.scalar_tensor_tensor(
-                out=u[t][:], in0=a_sq[t][:], scalar=1.0, in1=gT[t][:].rearrange(BY_WORD), op0=ALU.subtract, op1=ALU.mult
+                out=u[:], in0=a_sq[t][:], scalar=1.0, in1=gT[t][:].rearrange(BY_WORD), op0=ALU.subtract, op1=ALU.mult
             )
-
-        def finish_da_and_df(t):
+            x8 = work.tile([P, P, PACK], F32, name="x8", tag="x8")
+            nc.vector.scalar_tensor_tensor(
+                out=x8[:], in0=f_sq[t][:], scalar=1.0, in1=xT[t][:].rearrange(BY_WORD), op0=ALU.subtract, op1=ALU.mult
+            )
             grads[t] = work.tile([P, 2, P, PACK], BF16, name="grads", tag="grads", align_bytes=64)
             nc.vector.scalar_tensor_tensor(
-                out=grads[t][:, 1, :, :], in0=eT[t][:].rearrange(BY_WORD), scalar=1.0, in1=u[t][:],
+                out=grads[t][:, 1, :, :], in0=eT[t][:].rearrange(BY_WORD), scalar=1.0, in1=u[:],
                 op0=ALU.subtract, op1=ALU.mult,
             )
-            nc.vector.scalar_tensor_tensor(
-                out=grads[t][:, 0, :, :], in0=f_sq[t][:], scalar=1.0, in1=xT[t][:].rearrange(BY_WORD),
-                op0=ALU.subtract, op1=ALU.mult,
-            )
+            nc.vector.tensor_tensor(out=grads[t][:, 0, :, :], in0=mT[t][:].rearrange(BY_WORD), in1=x8[:], op=ALU.mult)
 
         def quantise_gradients(t):
             grad_codes[t] = work.tile([P, 2 * P], U32, name="grad_codes", tag="grad_codes", align_bytes=64)
@@ -193,29 +194,33 @@ def tile_ltccell_t_v_kernel(
             nc.vector.tensor_tensor(out=g_signed[t][:], in0=row(g_blk, t), in1=sign_f[t][:], op=ALU.mult)
 
         def times_delta_and_gradient(t, x5):
-            x7 = work.tile([P, HIDDEN], F32, name="x7", tag="x7")
+            x7[t] = work.tile([P, HIDDEN], F32, name="x7", tag="x7")
             nc.vector.scalar_tensor_tensor(
-                out=x7[:], in0=x5[:], scalar=minus_delta[:, t : t + 1], in1=g_signed[t][:],
+                out=x7[t][:], in0=x5[:], scalar=minus_delta[:, t : t + 1], in1=g_signed[t][:],
                 op0=ALU.mult, op1=ALU.mult,
             )
-            return x7
 
-        def times_state_difference(t, x7):
-            x9[t] = work.tile([P, HIDDEN], F32, name="x9", tag="x9")
-            nc.vector.tensor_tensor(out=x9[t][:], in0=x7[:], in1=m_rows[t][:], op=ALU.mult)
-
-        def a_minus_h_plus_bias(t):
-            m_rows[t] = work.tile([P, HIDDEN], F32, name="m_rows", tag="m_rows")
-            nc.gpsimd.tensor_tensor(out=m_rows[t][:], in0=row(a_blk, t), in1=row(h_blk, t), op=ALU.subtract)
-            nc.gpsimd.tensor_tensor(out=m_rows[t][:], in0=m_rows[t][:], in1=bias_rows[:], op=ALU.add)
+        def negate_h(t):
+            minus_h[t] = work.tile([P, HIDDEN], F32, name="minus_h", tag="minus_h")
+            nc.gpsimd.tensor_scalar(
+                out=minus_h[t][:], in0=row(h_blk, t), scalar1=-1.0, scalar2=0.0, op0=ALU.mult, op1=ALU.add
+            )
 
         def flip_factors(t):
             gT[t] = psum.tile([P, PACK, P], BF16, name="gT", tag="gT")
             flip(gT[t], row(g_blk, t), ident_bf16)
+            xT[t] = psum.tile([P, PACK, P], F32, name="xT", tag="xT")
+            flip(xT[t], x7[t], ident_f32)
             eT[t] = psum.tile([P, PACK, P], F32, name="eT", tag="eT")
             flip(eT[t], decay[t], ident_f32)
-            xT[t] = psum.tile([P, PACK, P], F32, name="xT", tag="xT")
-            flip(xT[t], x9[t], ident_f32)
+            mT[t] = psum.tile([P, PACK, P], F32, name="mT", tag="mT")
+            terms = (row(a_blk, t), minus_h[t], bias_rows)
+            for j in range(PACK):
+                for n, term in enumerate(terms):
+                    nc.tensor.matmul(
+                        out=mT[t][:, j, :], lhsT=term[:, j * P : (j + 1) * P], rhs=ident_f32[:], is_transpose=True,
+                        start=(n == 0), stop=(n == len(terms) - 1),
+                    )
 
         def multiply(t):
             acc[t] = psum.tile([P, OUT_FEATURES], F32, name="acc", tag="acc", bufs=2)
@@ -253,20 +258,16 @@ def tile_ltccell_t_v_kernel(
                 for n in range(CHAIN_OPS * (s % GROUP), CHAIN_OPS * (s % GROUP + 1)):
                     chain_op(s // GROUP + 1, n)
             if is_tile(s):
-                sign_the_gradient(s)
                 x5 = decay_times_ratio(s)
+                sign_the_gradient(s)
             if is_tile(s + PREP_AHEAD):
                 clear_sign(s + PREP_AHEAD)
             if is_tile(s):
-                x7 = times_delta_and_gradient(s, x5)
+                times_delta_and_gradient(s, x5)
             if is_tile(s + 1):
-                a_minus_h_plus_bias(s + 1)
+                negate_h(s + 1)
             if is_tile(s - 1):
-                gradient_times_a_factor(s - 1)
-            if is_tile(s):
-                times_state_difference(s, x7)
-            if is_tile(s - 1):
-                finish_da_and_df(s - 1)
+                finish_gradients(s - 1)
             if is_tile(s + PREP_AHEAD):
                 add_inv_tau(s + PREP_AHEAD)
             if is_tile(s - 1):

@@ -1,4 +1,3 @@
-import math
 from contextlib import ExitStack
 
 import concourse.mybir as mybir
@@ -17,12 +16,11 @@ ALU = mybir.AluOpType
 P = 128
 TOKENS, HIDDEN, OUT_FEATURES = 4096, 512, 512
 EPS = 1e-6
+SQRT_EPS = 1e-3
 TILES = TOKENS // P
 PACK = HIDDEN // P
+PAIRS = HIDDEN // 2 // P
 BLOCK = 4
-GROUP = 8
-CHAIN_OPS = 4
-PREP_AHEAD = 2 * GROUP - 1
 LOAD_AHEAD = 4
 
 FLOPS = 2 * TOKENS * OUT_FEATURES * 2 * HIDDEN
@@ -45,45 +43,74 @@ def tile_ltccell_t_v_kernel(
     with ExitStack() as stack:
         stack.enter_context(tc.manual_schedule())
         const = stack.enter_context(tc.tile_pool(name="const", bufs=1))
-        setup = stack.enter_context(tc.tile_pool(name="setup", bufs=2))
         work = stack.enter_context(tc.tile_pool(name="work", bufs=2))
         psum = stack.enter_context(tc.psum_pool(name="psum", bufs=1))
+
+        f_blk, a_blk, h_blk, g_blk, out_blk = {}, {}, {}, {}, {}
+
+        def load(blocks, rows, dtype, b, label, pieces):
+            blocks[b] = work.tile([P, BLOCK, HIDDEN], dtype, name=label, tag=label, bufs=3)
+            size = BLOCK // pieces
+            for i in range(0, BLOCK, size):
+                t = b * BLOCK + i
+                nc.sync.dma_start(out=blocks[b][:, i : i + size, :], in_=rows[:, t : t + size, :])
+
+        def row(blocks, t):
+            return blocks[t // BLOCK][:, t % BLOCK, :]
+
+        log_tau_4 = const.tile([P, P], BF16, name="log_tau_4")
+        nc.vector.memset(log_tau_4[:], 0.0)
+        nc.scalar.dma_start(out=log_tau_4[0:PACK, :], in_=log_tau.rearrange("(j p) -> j p", p=P))
+        delta = const.tile([P, TILES], BF16, name="delta")
+        nc.scalar.dma_start(out=delta[:], in_=time_delta.rearrange("(p t) o -> p (t o)", t=TILES))
+        bias_rows = const.tile([P, HIDDEN], BF16, name="bias_rows")
+
+        load(f_blk, f_rows, F32, 0, "f_blk", BLOCK)
+
+        w_raw = {}
+        for label, w in (("mod", W_mod), ("tgt", W_tgt)):
+            w_raw[label] = const.tile([P, PACK, HIDDEN], BF16, name="w_raw_" + label)
+            nc.scalar.dma_start(out=w_raw[label][:], in_=w[0:OUT_FEATURES, :].rearrange("(c p) k -> p c k", p=P))
+        nc.scalar.dma_start(out=bias_rows[:], in_=bias.partition_broadcast(P))
+
+        load(a_blk, a_rows, F32, 0, "a_blk", BLOCK)
+        load(g_blk, g_rows, BF16, 0, "g_blk", 2)
+        load(h_blk, h_rows, BF16, 0, "h_blk", 2)
 
         ident_f32 = const.tile([P, P], F32, name="ident_f32")
         make_identity(nc, ident_f32[:])
         ident_bf16 = const.tile([P, P], BF16, name="ident_bf16")
         make_identity(nc, ident_bf16[:])
 
-        log_tau_rows = const.tile([P, HIDDEN], BF16, name="log_tau_rows")
-        nc.scalar.dma_start(out=log_tau_rows[:], in_=log_tau.partition_broadcast(P))
-        delta = const.tile([P, TILES], BF16, name="delta")
-        nc.scalar.dma_start(out=delta[:], in_=time_delta.rearrange("(p t) o -> p (t o)", t=TILES))
-        bias_bf16 = const.tile([P, HIDDEN], BF16, name="bias_bf16")
-        nc.scalar.dma_start(out=bias_bf16[:], in_=bias.partition_broadcast(P))
-
-        inv_tau = const.tile([P, HIDDEN], F32, name="inv_tau")
-        nc.scalar.activation(out=inv_tau[:], in_=log_tau_rows[:], func=ACT.Exp, scale=-1.0)
-        bias_rows = const.tile([P, HIDDEN], F32, name="bias_rows")
-        nc.vector.tensor_copy(out=bias_rows[:], in_=bias_bf16[:])
         minus_delta = const.tile([P, TILES], F32, name="minus_delta")
         nc.vector.tensor_scalar(out=minus_delta[:], in0=delta[:], scalar1=-1.0, scalar2=None, op0=ALU.mult)
-        minus_delta_over_eps = const.tile([P, TILES], F32, name="minus_delta_over_eps")
-        nc.vector.tensor_scalar(
-            out=minus_delta_over_eps[:], in0=delta[:], scalar1=-1.0 / EPS, scalar2=None, op0=ALU.mult
-        )
 
-        def load_weight(w):
-            raw = setup.tile([P, PACK, HIDDEN], BF16, name="w_raw", tag="w_raw")
-            nc.scalar.dma_start(out=raw[:], in_=w[0:OUT_FEATURES, :].rearrange("(c p) k -> p c k", p=P))
-            return raw
+        lt_T = psum.tile([P, P], BF16, name="lt_T", tag="v")
+        nc.tensor.transpose(lt_T[:], log_tau_4[:], ident_bf16[:])
 
-        def quantise_weight(raw, label):
-            grouped = setup.tile([P, OUT_FEATURES, PACK], BF16, name="w_grouped", tag="w_grouped", align_bytes=64)
-            for c in range(OUT_FEATURES // P):
-                flipped = psum.tile([P, PACK, P], BF16, name="w_flipped", tag="gT")
-                for j in range(PACK):
-                    nc.tensor.transpose(flipped[:, j, :], raw[:, c, j * P : (j + 1) * P], ident_bf16[:])
-                nc.vector.tensor_copy(out=grouped[:, c * P : (c + 1) * P, :], in_=flipped[:].rearrange(BY_WORD))
+        def feature_tile(name):
+            return const.tile([P, PACK], F32, name=name)
+
+        clamped = feature_tile("clamped")
+        nc.vector.tensor_scalar(out=clamped[:], in0=lt_T[:, 0:PACK], scalar1=80.0, scalar2=None, op0=ALU.min)
+        tau = feature_tile("tau")
+        nc.scalar.activation(out=tau[:], in_=clamped[:], func=ACT.Exp)
+        den = feature_tile("den")
+        nc.vector.tensor_scalar(out=den[:], in0=tau[:], scalar1=EPS, scalar2=None, op0=ALU.add)
+        rate0 = feature_tile("rate0")
+        nc.vector.reciprocal(out=rate0[:], in_=den[:])
+        r0 = feature_tile("r0")
+        nc.vector.tensor_tensor(out=r0[:], in0=tau[:], in1=rate0[:], op=ALU.mult)
+        minus_r0 = feature_tile("minus_r0")
+        nc.vector.tensor_scalar(out=minus_r0[:], in0=r0[:], scalar1=-1.0, scalar2=None, op0=ALU.mult)
+        r0_sq = feature_tile("r0_sq")
+        nc.vector.tensor_tensor(out=r0_sq[:], in0=r0[:], in1=r0[:], op=ALU.mult)
+        minus_r0_sq = feature_tile("minus_r0_sq")
+        nc.vector.tensor_scalar(out=minus_r0_sq[:], in0=r0_sq[:], scalar1=-1.0, scalar2=None, op0=ALU.mult)
+        eps_r0_sq = feature_tile("eps_r0_sq")
+        nc.vector.tensor_scalar(out=eps_r0_sq[:], in0=r0_sq[:], scalar1=EPS, scalar2=None, op0=ALU.mult)
+
+        def quantise_weight(grouped, label):
             codes = const.tile([P, OUT_FEATURES], U32, name="codes_" + label, align_bytes=64)
             scales = const.tile([P, OUT_FEATURES], U8, name="scales_" + label, align_bytes=64)
             nc.vector.quantize_mx(
@@ -91,140 +118,160 @@ def tile_ltccell_t_v_kernel(
             )
             return codes, scales
 
-        raw_mod = load_weight(W_mod)
-        raw_tgt = load_weight(W_tgt)
+        def prepare_w_mod():
+            grouped = const.tile([P, OUT_FEATURES, PACK], BF16, name="w_grouped_mod", align_bytes=64)
+            for c in range(OUT_FEATURES // P):
+                flipped = psum.tile([P, PACK, P], BF16, name="w_flipped", tag="acc", bufs=2)
+                for j in range(PACK):
+                    nc.tensor.transpose(flipped[:, j, :], w_raw["mod"][:, c, j * P : (j + 1) * P], ident_bf16[:])
+                nc.vector.tensor_copy(out=grouped[:, c * P : (c + 1) * P, :], in_=flipped[:].rearrange(BY_WORD))
+            return grouped
 
-        s_tile, decay, sign_f = {}, {}, {}
-        f_blk, a_blk, h_blk, g_blk, out_blk = {}, {}, {}, {}, {}
-        f_sq, a_sq, minus_h, g_signed, x7 = {}, {}, {}, {}, {}
-        gT, eT, mT, xT = {}, {}, {}, {}
-        grads, grad_codes, grad_scales, acc = {}, {}, {}, {}
+        def prepare_w_tgt():
+            grouped = const.tile([P, OUT_FEATURES, PACK], BF16, name="w_grouped_tgt", align_bytes=64)
+            words = w_raw["tgt"][:].rearrange("p c k -> p (c k)").bitcast(F32)
+            pairs = grouped[:].rearrange("p i j -> p (i j)").bitcast(F32).rearrange("p (i u) -> p i u", u=PAIRS)
+            for c in range(OUT_FEATURES // P):
+                flipped = psum.tile([P, PAIRS, P], F32, name="w_flipped_words", tag="acc", bufs=2)
+                for u in range(PAIRS):
+                    first = c * HIDDEN // 2 + u * P
+                    nc.tensor.transpose(flipped[:, u, :], words[:, first : first + P], ident_f32[:])
+                nc.scalar.copy(out=pairs[:, c * P : (c + 1) * P, :], in_=flipped[:].rearrange(BY_WORD))
+            return grouped
 
-        def row(blocks, t):
-            return blocks[t // BLOCK][:, t % BLOCK, :]
+        minus_f, f_sq, sign_f, v, p2, decay, a_sq, u_rows, g_signed, x7, bias_h, w1 = ({} for n in range(12))
+        nxT, vT, xT, mT, daT, acc = ({} for n in range(6))
+        da, grads, grad_codes, grad_scales = ({} for n in range(4))
 
-        def flip(dst, src, ident):
-            for j in range(PACK):
-                nc.tensor.transpose(dst[:, j, :], src[:, j * P : (j + 1) * P], ident[:])
+        def make_minus_f(t):
+            minus_f[t] = work.tile([P, HIDDEN], F32, name="minus_f", tag="minus_f")
+            nc.vector.tensor_scalar(
+                out=minus_f[t][:].bitcast(I32), in0=row(f_blk, t).bitcast(I32), scalar1=-(2**31), scalar2=None,
+                op0=ALU.bitwise_or,
+            )
 
-        def load_f_for_d(t):
-            s_tile[t] = work.tile([P, HIDDEN], F32, name="s_tile", tag="s_tile", bufs=PREP_AHEAD + LOAD_AHEAD + 2)
-            nc.sync.dma_start(out=s_tile[t][:], in_=f_rows[:, t, :])
+        def make_f_sq(t):
+            f_sq[t] = work.tile([P, HIDDEN], F32, name="f_sq", tag="f_sq")
+            nc.scalar.activation(out=f_sq[t][:], in_=row(f_blk, t), func=ACT.Square, scale=SQRT_EPS)
 
-        def load_block(b):
-            tiles = slice(b * BLOCK, (b + 1) * BLOCK)
-            f_blk[b] = work.tile([P, BLOCK, HIDDEN], F32, name="f_blk", tag="f_blk", bufs=3)
-            nc.sync.dma_start(out=f_blk[b][:], in_=f_rows[:, tiles, :])
-            a_blk[b] = work.tile([P, BLOCK, HIDDEN], F32, name="a_blk", tag="a_blk", bufs=3)
-            nc.sync.dma_start(out=a_blk[b][:], in_=a_rows[:, tiles, :])
-            h_blk[b] = work.tile([P, BLOCK, HIDDEN], BF16, name="h_blk", tag="h_blk", bufs=3)
-            nc.sync.dma_start(out=h_blk[b][:], in_=h_rows[:, tiles, :])
-            g_blk[b] = work.tile([P, BLOCK, HIDDEN], BF16, name="g_blk", tag="g_blk", bufs=3)
-            nc.sync.dma_start(out=g_blk[b][:], in_=g_rows[:, tiles, :])
-
-        def clear_sign(t):
-            words = s_tile[t][:].bitcast(I32)
-            nc.vector.tensor_scalar(out=words, in0=words, scalar1=0x7FFFFFFF, scalar2=None, op0=ALU.bitwise_and)
-
-        def add_inv_tau(t):
-            nc.vector.tensor_tensor(out=s_tile[t][:], in0=s_tile[t][:], in1=inv_tau[:], op=ALU.add)
-
-        def chain_op(group, n):
-            first = group * GROUP
-            if n < GROUP:
-                t = first + n
-                nc.scalar.activation(out=s_tile[t][:], in_=s_tile[t][:], func=ACT.Ln)
-            elif n < 2 * GROUP:
-                t = first + n - GROUP
-                nc.scalar.activation(out=s_tile[t][:], in_=s_tile[t][:], func=ACT.Sigmoid, bias=math.log(EPS))
-            elif n % 2 == 0:
-                t = first + (n - 2 * GROUP) // 2
-                decay[t] = work.tile([P, HIDDEN], F32, name="decay", tag="decay", bufs=GROUP + 2)
-                nc.scalar.activation(
-                    out=decay[t][:], in_=s_tile[t][:], func=ACT.Exp, scale=minus_delta_over_eps[:, t : t + 1]
-                )
-            else:
-                t = first + (n - 2 * GROUP) // 2
-                nc.scalar.activation(out=s_tile[t][:], in_=s_tile[t][:], func=ACT.Square, scale=-1.0, bias=1.0)
-
-        def squares_and_sign(t):
-            sign_f[t] = work.tile([P, HIDDEN], BF16, name="sign_f", tag="sign_f", bufs=3)
+        def make_sign(t):
+            sign_f[t] = work.tile([P, HIDDEN], BF16, name="sign_f", tag="sign_f")
             nc.scalar.activation(out=sign_f[t][:], in_=row(f_blk, t), func=ACT.Sign)
-            fT = psum.tile([P, PACK, P], F32, name="fT", tag="fT")
-            flip(fT, row(f_blk, t), ident_f32)
-            aT = psum.tile([P, PACK, P], F32, name="aT", tag="aT")
-            flip(aT, row(a_blk, t), ident_f32)
-            f_sq[t] = work.tile([P, P, PACK], F32, name="f_sq", tag="f_sq", bufs=3)
-            nc.scalar.activation(out=f_sq[t][:], in_=fT[:].rearrange(BY_WORD), func=ACT.Square)
-            a_sq[t] = work.tile([P, P, PACK], F32, name="a_sq", tag="a_sq", bufs=3)
-            nc.scalar.activation(out=a_sq[t][:], in_=aT[:].rearrange(BY_WORD), func=ACT.Square)
 
-        def finish_gradients(t):
-            u = work.tile([P, P, PACK], F32, name="u", tag="u")
+        def flip_sum(dst, terms):
+            for j in range(PACK):
+                for n, term in enumerate(terms):
+                    nc.tensor.matmul(
+                        out=dst[:, j, :], lhsT=term[:, j * P : (j + 1) * P], rhs=ident_f32[:], is_transpose=True,
+                        start=(n == 0), stop=(n == len(terms) - 1),
+                    )
+
+        def flip_f(t):
+            nxT[t] = psum.tile([P, PACK, P], F32, name="nxT", tag="nxT", bufs=2)
+            flip_sum(nxT[t], (minus_f[t], f_sq[t]))
+
+        def make_rate(t):
+            v[t] = work.tile([P, PACK, P], F32, name="v", tag="v")
+            for j in range(PACK):
+                nc.scalar.activation(
+                    out=v[t][:, j, :], in_=nxT[t][:, j, :], func=ACT.Identity,
+                    scale=minus_r0_sq[:, j : j + 1], bias=rate0[:, j : j + 1],
+                )
+
+        def make_p2(t):
+            p2[t] = work.tile([P, PACK, P], F32, name="p2", tag="p2", bufs=5)
+            for j in range(PACK):
+                nc.scalar.activation(
+                    out=p2[t][:, j, :], in_=nxT[t][:, j, :], func=ACT.Square,
+                    scale=minus_r0[:, j : j + 1], bias=eps_r0_sq[:, j : j + 1],
+                )
+
+        def flip_rate(t):
+            vT[t] = psum.tile([P, HIDDEN], F32, name="vT", tag="v")
+            for j in range(PACK):
+                nc.tensor.transpose(vT[t][:, j * P : (j + 1) * P], v[t][:, j, :], ident_f32[:])
+
+        def make_decay(t):
+            decay[t] = work.tile([P, HIDDEN], F32, name="decay", tag="decay", bufs=3)
+            nc.scalar.activation(out=decay[t][:], in_=vT[t][:], func=ACT.Exp, scale=minus_delta[:, t : t + 1])
+
+        def make_a_sq(t):
+            a_sq[t] = work.tile([P, HIDDEN], F32, name="a_sq", tag="a_sq")
+            nc.scalar.activation(out=a_sq[t][:], in_=row(a_blk, t), func=ACT.Square)
+
+        def make_u(t):
+            u_rows[t] = work.tile([P, HIDDEN], F32, name="u_rows", tag="u_rows")
             nc.vector.scalar_tensor_tensor(
-                out=u[:], in0=a_sq[t][:], scalar=1.0, in1=gT[t][:].rearrange(BY_WORD), op0=ALU.subtract, op1=ALU.mult
+                out=u_rows[t][:], in0=a_sq[t][:], scalar=1.0, in1=row(g_blk, t), op0=ALU.subtract, op1=ALU.mult
             )
-            x8 = work.tile([P, P, PACK], F32, name="x8", tag="x8")
+
+        def make_g_signed(t):
+            g_signed[t] = work.tile([P, HIDDEN], BF16, name="g_signed", tag="g_signed")
+            nc.vector.tensor_tensor(out=g_signed[t][:], in0=row(g_blk, t), in1=sign_f[t][:], op=ALU.mult)
+
+        def make_x7(t):
+            x7[t] = work.tile([P, HIDDEN], F32, name="x7", tag="x7")
             nc.vector.scalar_tensor_tensor(
-                out=x8[:], in0=f_sq[t][:], scalar=1.0, in1=xT[t][:].rearrange(BY_WORD), op0=ALU.subtract, op1=ALU.mult
+                out=x7[t][:], in0=decay[t][:], scalar=minus_delta[:, t : t + 1], in1=g_signed[t][:],
+                op0=ALU.mult, op1=ALU.mult,
             )
-            grads[t] = work.tile([P, 2, P, PACK], BF16, name="grads", tag="grads", align_bytes=64)
+
+        def make_da(t):
+            da[t] = work.tile([P, HIDDEN], BF16, name="da", tag="da")
             nc.vector.scalar_tensor_tensor(
-                out=grads[t][:, 1, :, :], in0=eT[t][:].rearrange(BY_WORD), scalar=1.0, in1=u[:],
-                op0=ALU.subtract, op1=ALU.mult,
+                out=da[t][:], in0=decay[t][:], scalar=1.0, in1=u_rows[t][:], op0=ALU.subtract, op1=ALU.mult
             )
-            nc.vector.tensor_tensor(out=grads[t][:, 0, :, :], in0=mT[t][:].rearrange(BY_WORD), in1=x8[:], op=ALU.mult)
+
+        def flip_da(t):
+            daT[t] = psum.tile([P, PAIRS, P], F32, name="daT", tag="daT")
+            words = da[t][:].bitcast(F32)
+            for u in range(PAIRS):
+                nc.tensor.transpose(daT[t][:, u, :], words[:, u * P : (u + 1) * P], ident_f32[:])
+
+        def flip_x7(t):
+            xT[t] = psum.tile([P, PACK, P], F32, name="xT", tag="xT")
+            flip_sum(xT[t], (x7[t],))
+
+        def make_bias_h(t):
+            bias_h[t] = work.tile([P, HIDDEN], F32, name="bias_h", tag="bias_h")
+            nc.gpsimd.tensor_tensor(out=bias_h[t][:], in0=bias_rows[:], in1=row(h_blk, t), op=ALU.subtract)
+
+        def flip_m(t):
+            mT[t] = psum.tile([P, PACK, P], F32, name="mT", tag="mT")
+            flip_sum(mT[t], (row(a_blk, t), bias_h[t]))
+
+        def make_w1(t):
+            w1[t] = work.tile([P, PACK, P], F32, name="w1", tag="w1")
+            for j in range(PACK):
+                nc.vector.scalar_tensor_tensor(
+                    out=w1[t][:, j, :], in0=p2[t][:, j, :], scalar=r0_sq[:, j : j + 1], in1=xT[t][:, j, :],
+                    op0=ALU.subtract, op1=ALU.mult,
+                )
+
+        def regroup_da(t):
+            grads[t] = work.tile([P, 2, P * PACK], BF16, name="grads", tag="grads", align_bytes=64)
+            nc.vector.tensor_copy(
+                out=grads[t][:, 1, :].bitcast(F32).rearrange("p (t u) -> p t u", u=PAIRS),
+                in_=daT[t][:].rearrange(BY_WORD),
+            )
+
+        def make_df(t):
+            nc.vector.tensor_tensor(
+                out=grads[t][:, 0, :].rearrange("p (t j) -> p t j", j=PACK), in0=mT[t][:].rearrange(BY_WORD),
+                in1=w1[t][:].rearrange(BY_WORD), op=ALU.mult,
+            )
 
         def quantise_gradients(t):
             grad_codes[t] = work.tile([P, 2 * P], U32, name="grad_codes", tag="grad_codes", align_bytes=64)
             grad_scales[t] = work.tile([P, 2 * P], U8, name="grad_scales", tag="grad_scales", align_bytes=64)
             nc.vector.quantize_mx(
-                out=grad_codes[t][:].bitcast(E5M2_X4),
-                scales=grad_scales[t][:],
-                in_=grads[t][:].rearrange("p s t j -> p (s t j)"),
+                out=grad_codes[t][:].bitcast(E5M2_X4), scales=grad_scales[t][:],
+                in_=grads[t][:].rearrange("p s k -> p (s k)"),
             )
-
-        def decay_times_ratio(t):
-            x5 = work.tile([P, HIDDEN], F32, name="x5", tag="x5")
-            nc.vector.tensor_tensor(out=x5[:], in0=decay[t][:], in1=s_tile[t][:], op=ALU.mult)
-            return x5
-
-        def sign_the_gradient(t):
-            g_signed[t] = work.tile([P, HIDDEN], BF16, name="g_signed", tag="g_signed")
-            nc.vector.tensor_tensor(out=g_signed[t][:], in0=row(g_blk, t), in1=sign_f[t][:], op=ALU.mult)
-
-        def times_delta_and_gradient(t, x5):
-            x7[t] = work.tile([P, HIDDEN], F32, name="x7", tag="x7")
-            nc.vector.scalar_tensor_tensor(
-                out=x7[t][:], in0=x5[:], scalar=minus_delta[:, t : t + 1], in1=g_signed[t][:],
-                op0=ALU.mult, op1=ALU.mult,
-            )
-
-        def negate_h(t):
-            minus_h[t] = work.tile([P, HIDDEN], F32, name="minus_h", tag="minus_h")
-            nc.gpsimd.tensor_scalar(
-                out=minus_h[t][:], in0=row(h_blk, t), scalar1=-1.0, scalar2=0.0, op0=ALU.mult, op1=ALU.add
-            )
-
-        def flip_factors(t):
-            gT[t] = psum.tile([P, PACK, P], BF16, name="gT", tag="gT")
-            flip(gT[t], row(g_blk, t), ident_bf16)
-            xT[t] = psum.tile([P, PACK, P], F32, name="xT", tag="xT")
-            flip(xT[t], x7[t], ident_f32)
-            eT[t] = psum.tile([P, PACK, P], F32, name="eT", tag="eT")
-            flip(eT[t], decay[t], ident_f32)
-            mT[t] = psum.tile([P, PACK, P], F32, name="mT", tag="mT")
-            terms = (row(a_blk, t), minus_h[t], bias_rows)
-            for j in range(PACK):
-                for n, term in enumerate(terms):
-                    nc.tensor.matmul(
-                        out=mT[t][:, j, :], lhsT=term[:, j * P : (j + 1) * P], rhs=ident_f32[:], is_transpose=True,
-                        start=(n == 0), stop=(n == len(terms) - 1),
-                    )
 
         def multiply(t):
             acc[t] = psum.tile([P, OUT_FEATURES], F32, name="acc", tag="acc", bufs=2)
-            for n, (codes, scales) in enumerate((weight_mod, weight_tgt)):
+            for n, (codes, scales) in enumerate(weights):
                 tokens = slice(n * P, (n + 1) * P)
                 nc.tensor.matmul_mx(
                     out=acc[t][:],
@@ -236,52 +283,63 @@ def tile_ltccell_t_v_kernel(
                     stop=(n == 1),
                 )
 
-        def store(t):
+        def copy_out(t):
             b = t // BLOCK
             if t % BLOCK == 0:
                 out_blk[b] = work.tile([P, BLOCK, OUT_FEATURES], F32, name="out_blk", tag="out_blk")
             nc.scalar.copy(out=row(out_blk, t), in_=acc[t][:])
-            if t % BLOCK == BLOCK - 1:
+
+        def store(t):
+            b = t // BLOCK
+            if b == TILES // BLOCK - 1:
+                nc.sync.dma_start(out=out_rows[:, t : t + 1, :], in_=out_blk[b][:, t % BLOCK : t % BLOCK + 1, :])
+            elif t % BLOCK == BLOCK - 1:
                 nc.sync.dma_start(out=out_rows[:, b * BLOCK : (b + 1) * BLOCK, :], in_=out_blk[b][:])
 
-        def is_tile(t):
-            return 0 <= t < TILES
+        def on(stage, t):
+            if 0 <= t < TILES:
+                stage(t)
+
+        def load_block(first_use, blocks, rows, dtype, label):
+            t = first_use + LOAD_AHEAD
+            if t % BLOCK == 0 and BLOCK <= t < TILES:
+                load(blocks, rows, dtype, t // BLOCK, label, 1)
 
         def step(s):
-            if is_tile(s + PREP_AHEAD + LOAD_AHEAD):
-                load_f_for_d(s + PREP_AHEAD + LOAD_AHEAD)
-            if (s + 1 + BLOCK) % BLOCK == 0 and is_tile(s + 1 + BLOCK):
-                load_block((s + 1 + BLOCK) // BLOCK)
-            if is_tile(s + 1):
-                squares_and_sign(s + 1)
-            if is_tile((s // GROUP + 1) * GROUP):
-                for n in range(CHAIN_OPS * (s % GROUP), CHAIN_OPS * (s % GROUP + 1)):
-                    chain_op(s // GROUP + 1, n)
-            if is_tile(s):
-                x5 = decay_times_ratio(s)
-                sign_the_gradient(s)
-            if is_tile(s + PREP_AHEAD):
-                clear_sign(s + PREP_AHEAD)
-            if is_tile(s):
-                times_delta_and_gradient(s, x5)
-            if is_tile(s + 1):
-                negate_h(s + 1)
-            if is_tile(s - 1):
-                finish_gradients(s - 1)
-            if is_tile(s + PREP_AHEAD):
-                add_inv_tau(s + PREP_AHEAD)
-            if is_tile(s - 1):
-                quantise_gradients(s - 1)
-            if is_tile(s):
-                flip_factors(s)
-            if is_tile(s - 1):
-                multiply(s - 1)
-            if is_tile(s - 2):
-                store(s - 2)
+            load_block(s + 3, f_blk, f_rows, F32, "f_blk")
+            load_block(s + 2, a_blk, a_rows, F32, "a_blk")
+            load_block(s + 1, g_blk, g_rows, BF16, "g_blk")
+            load_block(s + 1, h_blk, h_rows, BF16, "h_blk")
+            on(multiply, s - 2)
+            on(make_decay, s + 1)
+            on(make_rate, s + 2)
+            on(make_p2, s + 2)
+            on(make_x7, s)
+            on(regroup_da, s - 1)
+            on(make_da, s)
+            on(make_w1, s - 1)
+            on(make_minus_f, s + 3)
+            on(make_f_sq, s + 3)
+            on(make_a_sq, s + 2)
+            on(make_sign, s + 2)
+            on(copy_out, s - 2)
+            on(make_bias_h, s + 1)
+            on(make_df, s - 1)
+            on(make_u, s + 1)
+            on(make_g_signed, s + 1)
+            on(quantise_gradients, s - 1)
+            on(flip_rate, s + 2)
+            on(flip_da, s)
+            on(flip_x7, s)
+            on(flip_m, s)
+            on(flip_f, s + 3)
+            on(store, s - 2)
 
-        for s in range(-(PREP_AHEAD + LOAD_AHEAD), 0):
-            step(s)
-        weight_mod = quantise_weight(raw_mod, "mod")
-        weight_tgt = quantise_weight(raw_tgt, "tgt")
+        step(-3)
+        grouped_tgt = prepare_w_tgt()
+        grouped_mod = prepare_w_mod()
+        step(-2)
+        weights = [quantise_weight(grouped_mod, "mod"), quantise_weight(grouped_tgt, "tgt")]
+        step(-1)
         for s in range(0, TILES + 2):
             step(s)

@@ -158,17 +158,18 @@ def tile_ltccell_t_v_kernel(
             sign_f[t] = work.tile([P, HIDDEN], BF16, name="sign_f", tag="sign_f")
             nc.scalar.activation(out=sign_f[t][:], in_=row(f_blk, t), func=ACT.Sign)
 
-        def flip_sum(dst, terms):
+        def flip_sum(dst, terms, plain=0):
             for j in range(PACK):
                 for n, term in enumerate(terms):
+                    last = n == len(terms) - 1
                     nc.tensor.matmul(
-                        out=dst[:, j, :], lhsT=term[:, j * P : (j + 1) * P], rhs=ident_f32[:], is_transpose=True,
-                        start=(n == 0), stop=(n == len(terms) - 1),
+                        out=dst[:, j, :], lhsT=term[:, j * P : (j + 1) * P], rhs=ident_f32[:],
+                        is_transpose=not (last and j < plain), start=(n == 0), stop=last,
                     )
 
         def flip_f(t):
             nxT[t] = psum.tile([P, PACK, P], F32, name="nxT", tag="nxT", bufs=2)
-            flip_sum(nxT[t], (minus_f[t], f_sq[t]))
+            flip_sum(nxT[t], (minus_f[t], f_sq[t]), plain=3)
 
         def make_rate(t):
             v[t] = work.tile([P, PACK, P], F32, name="v", tag="v")
@@ -310,7 +311,6 @@ def tile_ltccell_t_v_kernel(
             load_block(s + 2, a_blk, a_rows, F32, "a_blk")
             load_block(s + 1, g_blk, g_rows, BF16, "g_blk")
             load_block(s + 1, h_blk, h_rows, BF16, "h_blk")
-            on(multiply, s - 2)
             on(make_decay, s + 1)
             on(make_rate, s + 2)
             on(make_p2, s + 2)
@@ -322,7 +322,6 @@ def tile_ltccell_t_v_kernel(
             on(make_f_sq, s + 3)
             on(make_a_sq, s + 2)
             on(make_sign, s + 2)
-            on(copy_out, s - 2)
             on(make_bias_h, s + 1)
             on(make_df, s - 1)
             on(make_u, s + 1)
@@ -330,6 +329,8 @@ def tile_ltccell_t_v_kernel(
             on(quantise_gradients, s - 1)
             on(flip_rate, s + 2)
             on(flip_da, s)
+            on(multiply, s - 2)
+            on(copy_out, s - 2)
             on(flip_x7, s)
             on(flip_m, s)
             on(flip_f, s + 3)

@@ -64,51 +64,42 @@ def tile_ltccell_t_v_kernel(
         delta = const.tile([P, TILES], BF16, name="delta")
         nc.scalar.dma_start(out=delta[:], in_=time_delta.rearrange("(p t) o -> p (t o)", t=TILES))
         bias_rows = const.tile([P, HIDDEN], BF16, name="bias_rows")
+        w_raw = {label: const.tile([P, PACK, HIDDEN], BF16, name="w_raw_" + label) for label in ("mod", "tgt")}
+
+        def load_weight(label, w):
+            nc.sync.dma_start(out=w_raw[label][:], in_=w[0:OUT_FEATURES, :].rearrange("(c p) k -> p c k", p=P))
 
         load(f_blk, f_rows, F32, 0, "f_blk", BLOCK)
-
-        w_raw = {}
-        for label, w in (("mod", W_mod), ("tgt", W_tgt)):
-            w_raw[label] = const.tile([P, PACK, HIDDEN], BF16, name="w_raw_" + label)
-            nc.scalar.dma_start(out=w_raw[label][:], in_=w[0:OUT_FEATURES, :].rearrange("(c p) k -> p c k", p=P))
-        nc.scalar.dma_start(out=bias_rows[:], in_=bias.partition_broadcast(P))
-
         load(a_blk, a_rows, F32, 0, "a_blk", BLOCK)
+        load_weight("tgt", W_tgt)
         load(g_blk, g_rows, BF16, 0, "g_blk", 2)
+        load_weight("mod", W_mod)
         load(h_blk, h_rows, BF16, 0, "h_blk", 2)
 
         ident_f32 = const.tile([P, P], F32, name="ident_f32")
         make_identity(nc, ident_f32[:])
         ident_bf16 = const.tile([P, P], BF16, name="ident_bf16")
         make_identity(nc, ident_bf16[:])
+        nc.gpsimd.dma_start(out=bias_rows[:], in_=bias.partition_broadcast(P))
 
+        clamped, tau, den, rate0, r0, minus_r0, r0_sq, minus_r0_sq, eps_r0_sq = (
+            const.tile([P, PACK], F32, name="feature_%d" % n) for n in range(9)
+        )
         minus_delta = const.tile([P, TILES], F32, name="minus_delta")
-        nc.vector.tensor_scalar(out=minus_delta[:], in0=delta[:], scalar1=-1.0, scalar2=None, op0=ALU.mult)
 
-        lt_T = psum.tile([P, P], BF16, name="lt_T", tag="v")
-        nc.tensor.transpose(lt_T[:], log_tau_4[:], ident_bf16[:])
-
-        def feature_tile(name):
-            return const.tile([P, PACK], F32, name=name)
-
-        clamped = feature_tile("clamped")
-        nc.vector.tensor_scalar(out=clamped[:], in0=lt_T[:, 0:PACK], scalar1=80.0, scalar2=None, op0=ALU.min)
-        tau = feature_tile("tau")
-        nc.scalar.activation(out=tau[:], in_=clamped[:], func=ACT.Exp)
-        den = feature_tile("den")
-        nc.vector.tensor_scalar(out=den[:], in0=tau[:], scalar1=EPS, scalar2=None, op0=ALU.add)
-        rate0 = feature_tile("rate0")
-        nc.vector.reciprocal(out=rate0[:], in_=den[:])
-        r0 = feature_tile("r0")
-        nc.vector.tensor_tensor(out=r0[:], in0=tau[:], in1=rate0[:], op=ALU.mult)
-        minus_r0 = feature_tile("minus_r0")
-        nc.vector.tensor_scalar(out=minus_r0[:], in0=r0[:], scalar1=-1.0, scalar2=None, op0=ALU.mult)
-        r0_sq = feature_tile("r0_sq")
-        nc.vector.tensor_tensor(out=r0_sq[:], in0=r0[:], in1=r0[:], op=ALU.mult)
-        minus_r0_sq = feature_tile("minus_r0_sq")
-        nc.vector.tensor_scalar(out=minus_r0_sq[:], in0=r0_sq[:], scalar1=-1.0, scalar2=None, op0=ALU.mult)
-        eps_r0_sq = feature_tile("eps_r0_sq")
-        nc.vector.tensor_scalar(out=eps_r0_sq[:], in0=r0_sq[:], scalar1=EPS, scalar2=None, op0=ALU.mult)
+        def make_feature_numbers():
+            lt_T = psum.tile([P, P], BF16, name="lt_T", tag="v")
+            nc.tensor.transpose(lt_T[:], log_tau_4[:], ident_bf16[:])
+            nc.vector.tensor_scalar(out=clamped[:], in0=lt_T[:, 0:PACK], scalar1=80.0, scalar2=None, op0=ALU.min)
+            nc.scalar.activation(out=tau[:], in_=clamped[:], func=ACT.Exp)
+            nc.vector.tensor_scalar(out=den[:], in0=tau[:], scalar1=EPS, scalar2=None, op0=ALU.add)
+            nc.vector.reciprocal(out=rate0[:], in_=den[:])
+            nc.vector.tensor_tensor(out=r0[:], in0=tau[:], in1=rate0[:], op=ALU.mult)
+            nc.vector.tensor_scalar(out=minus_r0[:], in0=r0[:], scalar1=-1.0, scalar2=None, op0=ALU.mult)
+            nc.vector.tensor_tensor(out=r0_sq[:], in0=r0[:], in1=r0[:], op=ALU.mult)
+            nc.vector.tensor_scalar(out=minus_r0_sq[:], in0=r0_sq[:], scalar1=-1.0, scalar2=None, op0=ALU.mult)
+            nc.vector.tensor_scalar(out=eps_r0_sq[:], in0=r0_sq[:], scalar1=EPS, scalar2=None, op0=ALU.mult)
+            nc.vector.tensor_scalar(out=minus_delta[:], in0=delta[:], scalar1=-1.0, scalar2=None, op0=ALU.mult)
 
         def quantise_weight(grouped, label):
             codes = const.tile([P, OUT_FEATURES], U32, name="codes_" + label, align_bytes=64)
@@ -250,13 +241,13 @@ def tile_ltccell_t_v_kernel(
                 )
 
         def regroup_da(t):
-            grads[t] = work.tile([P, 2, P * PACK], BF16, name="grads", tag="grads", align_bytes=64)
             nc.vector.tensor_copy(
                 out=grads[t][:, 1, :].bitcast(F32).rearrange("p (t u) -> p t u", u=PAIRS),
                 in_=daT[t][:].rearrange(BY_WORD),
             )
 
         def make_df(t):
+            grads[t] = work.tile([P, 2, P * PACK], BF16, name="grads", tag="grads", align_bytes=64)
             nc.vector.tensor_tensor(
                 out=grads[t][:, 0, :].rearrange("p (t j) -> p t j", j=PACK), in0=mT[t][:].rearrange(BY_WORD),
                 in1=w1[t][:].rearrange(BY_WORD), op=ALU.mult,
@@ -311,36 +302,37 @@ def tile_ltccell_t_v_kernel(
             load_block(s + 2, a_blk, a_rows, F32, "a_blk")
             load_block(s + 1, g_blk, g_rows, BF16, "g_blk")
             load_block(s + 1, h_blk, h_rows, BF16, "h_blk")
+            on(make_f_sq, s + 3)
             on(make_decay, s + 1)
             on(make_rate, s + 2)
             on(make_p2, s + 2)
             on(make_x7, s)
-            on(regroup_da, s - 1)
             on(make_da, s)
-            on(make_w1, s - 1)
             on(make_minus_f, s + 3)
-            on(make_f_sq, s + 3)
+            on(make_w1, s - 1)
             on(make_a_sq, s + 2)
             on(make_sign, s + 2)
+            on(copy_out, s - 2)
             on(make_bias_h, s + 1)
-            on(make_df, s - 1)
             on(make_u, s + 1)
+            on(make_df, s - 1)
+            on(regroup_da, s - 1)
             on(make_g_signed, s + 1)
             on(quantise_gradients, s - 1)
-            on(flip_rate, s + 2)
-            on(flip_da, s)
-            on(multiply, s - 2)
-            on(copy_out, s - 2)
+            on(flip_f, s + 3)
             on(flip_x7, s)
             on(flip_m, s)
-            on(flip_f, s + 3)
+            on(flip_da, s)
+            on(flip_rate, s + 2)
+            on(multiply, s - 1)
             on(store, s - 2)
 
         step(-3)
-        grouped_tgt = prepare_w_tgt()
-        grouped_mod = prepare_w_mod()
+        make_feature_numbers()
         step(-2)
-        weights = [quantise_weight(grouped_mod, "mod"), quantise_weight(grouped_tgt, "tgt")]
+        grouped_tgt = prepare_w_tgt()
         step(-1)
+        grouped_mod = prepare_w_mod()
+        weights = [quantise_weight(grouped_mod, "mod"), quantise_weight(grouped_tgt, "tgt")]
         for s in range(0, TILES + 2):
             step(s)

@@ -60,7 +60,7 @@ def tile_ltccell_t_v_kernel(
 
         log_tau_4 = const.tile([P, P], BF16, name="log_tau_4")
         nc.vector.memset(log_tau_4[:], 0.0)
-        nc.scalar.dma_start(out=log_tau_4[0:PACK, :], in_=log_tau.rearrange("(j p) -> j p", p=P))
+        nc.sync.dma_start(out=log_tau_4[0:PACK, :], in_=log_tau.rearrange("(j p) -> j p", p=P))
         delta = const.tile([P, TILES], BF16, name="delta")
         nc.scalar.dma_start(out=delta[:], in_=time_delta.rearrange("(p t) o -> p (t o)", t=TILES))
         bias_rows = const.tile([P, HIDDEN], BF16, name="bias_rows")
@@ -69,12 +69,30 @@ def tile_ltccell_t_v_kernel(
         def load_weight(label, w):
             nc.sync.dma_start(out=w_raw[label][:], in_=w[0:OUT_FEATURES, :].rearrange("(c p) k -> p c k", p=P))
 
-        load(f_blk, f_rows, F32, 0, "f_blk", BLOCK)
-        load(a_blk, a_rows, F32, 0, "a_blk", BLOCK)
+        def load_first(blocks, rows, dtype, label):
+            blocks[0] = work.tile([P, BLOCK, HIDDEN], dtype, name=label, tag=label, bufs=3)
+            return lambda t: nc.sync.dma_start(out=blocks[0][:, t : t + 1, :], in_=rows[:, t : t + 1, :])
+
+        load_f = load_first(f_blk, f_rows, F32, "f_blk")
+        load_a = load_first(a_blk, a_rows, F32, "a_blk")
+        load_g = load_first(g_blk, g_rows, BF16, "g_blk")
+        load_h = load_first(h_blk, h_rows, BF16, "h_blk")
+        load_f(0)
         load_weight("tgt", W_tgt)
-        load(g_blk, g_rows, BF16, 0, "g_blk", 2)
+        load_f(1)
         load_weight("mod", W_mod)
-        load(h_blk, h_rows, BF16, 0, "h_blk", 2)
+        load_a(0)
+        load_g(0)
+        load_f(2)
+        load_h(0)
+        load_a(1)
+        load_g(1)
+        load_h(1)
+        load_f(3)
+        for t in range(2, BLOCK):
+            load_a(t)
+            load_g(t)
+            load_h(t)
 
         ident_f32 = const.tile([P, P], F32, name="ident_f32")
         make_identity(nc, ident_f32[:])
@@ -87,9 +105,10 @@ def tile_ltccell_t_v_kernel(
         )
         minus_delta = const.tile([P, TILES], F32, name="minus_delta")
 
+        lt_T = psum.tile([P, P], BF16, name="lt_T", tag="v")
+        nc.tensor.transpose(lt_T[:], log_tau_4[:], ident_bf16[:])
+
         def make_feature_numbers():
-            lt_T = psum.tile([P, P], BF16, name="lt_T", tag="v")
-            nc.tensor.transpose(lt_T[:], log_tau_4[:], ident_bf16[:])
             nc.vector.tensor_scalar(out=clamped[:], in0=lt_T[:, 0:PACK], scalar1=80.0, scalar2=None, op0=ALU.min)
             nc.scalar.activation(out=tau[:], in_=clamped[:], func=ACT.Exp)
             nc.vector.tensor_scalar(out=den[:], in0=tau[:], scalar1=EPS, scalar2=None, op0=ALU.add)
@@ -127,7 +146,7 @@ def tile_ltccell_t_v_kernel(
                 for u in range(PAIRS):
                     first = c * HIDDEN // 2 + u * P
                     nc.tensor.transpose(flipped[:, u, :], words[:, first : first + P], ident_f32[:])
-                nc.scalar.copy(out=pairs[:, c * P : (c + 1) * P, :], in_=flipped[:].rearrange(BY_WORD))
+                nc.vector.tensor_copy(out=pairs[:, c * P : (c + 1) * P, :], in_=flipped[:].rearrange(BY_WORD))
             return grouped
 
         minus_f, f_sq, sign_f, v, p2, decay, a_sq, u_rows, g_signed, x7, bias_h, w1 = ({} for n in range(12))
@@ -160,7 +179,7 @@ def tile_ltccell_t_v_kernel(
 
         def flip_f(t):
             nxT[t] = psum.tile([P, PACK, P], F32, name="nxT", tag="nxT", bufs=2)
-            flip_sum(nxT[t], (minus_f[t], f_sq[t]), plain=3)
+            flip_sum(nxT[t], (minus_f[t], f_sq[t]), plain=3 if t >= BLOCK - 1 else 0)
 
         def make_rate(t):
             v[t] = work.tile([P, PACK, P], F32, name="v", tag="v")
@@ -188,8 +207,8 @@ def tile_ltccell_t_v_kernel(
             nc.scalar.activation(out=decay[t][:], in_=vT[t][:], func=ACT.Exp, scale=minus_delta[:, t : t + 1])
 
         def make_a_sq(t):
-            a_sq[t] = work.tile([P, HIDDEN], F32, name="a_sq", tag="a_sq")
-            nc.scalar.activation(out=a_sq[t][:], in_=row(a_blk, t), func=ACT.Square)
+            a_sq[t] = work.tile([P, HIDDEN], F32, name="a_sq", tag="a_sq", bufs=3)
+            nc.gpsimd.tensor_tensor(out=a_sq[t][:], in0=row(a_blk, t), in1=row(a_blk, t), op=ALU.mult)
 
         def make_u(t):
             u_rows[t] = work.tile([P, HIDDEN], F32, name="u_rows", tag="u_rows")
@@ -225,7 +244,7 @@ def tile_ltccell_t_v_kernel(
             flip_sum(xT[t], (x7[t],))
 
         def make_bias_h(t):
-            bias_h[t] = work.tile([P, HIDDEN], F32, name="bias_h", tag="bias_h")
+            bias_h[t] = work.tile([P, HIDDEN], F32, name="bias_h", tag="bias_h", bufs=3)
             nc.gpsimd.tensor_tensor(out=bias_h[t][:], in0=bias_rows[:], in1=row(h_blk, t), op=ALU.subtract)
 
         def flip_m(t):
@@ -241,13 +260,13 @@ def tile_ltccell_t_v_kernel(
                 )
 
         def regroup_da(t):
-            nc.vector.tensor_copy(
+            grads[t] = work.tile([P, 2, P * PACK], BF16, name="grads", tag="grads", align_bytes=64)
+            nc.scalar.copy(
                 out=grads[t][:, 1, :].bitcast(F32).rearrange("p (t u) -> p t u", u=PAIRS),
                 in_=daT[t][:].rearrange(BY_WORD),
             )
 
         def make_df(t):
-            grads[t] = work.tile([P, 2, P * PACK], BF16, name="grads", tag="grads", align_bytes=64)
             nc.vector.tensor_tensor(
                 out=grads[t][:, 0, :].rearrange("p (t j) -> p t j", j=PACK), in0=mT[t][:].rearrange(BY_WORD),
                 in1=w1[t][:].rearrange(BY_WORD), op=ALU.mult,
@@ -306,17 +325,17 @@ def tile_ltccell_t_v_kernel(
             on(make_decay, s + 1)
             on(make_rate, s + 2)
             on(make_p2, s + 2)
+            on(regroup_da, s - 1)
             on(make_x7, s)
             on(make_da, s)
             on(make_minus_f, s + 3)
             on(make_w1, s - 1)
-            on(make_a_sq, s + 2)
             on(make_sign, s + 2)
             on(copy_out, s - 2)
             on(make_bias_h, s + 1)
+            on(make_a_sq, s + 2)
             on(make_u, s + 1)
             on(make_df, s - 1)
-            on(regroup_da, s - 1)
             on(make_g_signed, s + 1)
             on(quantise_gradients, s - 1)
             on(flip_f, s + 3)
@@ -329,10 +348,11 @@ def tile_ltccell_t_v_kernel(
 
         step(-3)
         make_feature_numbers()
-        step(-2)
         grouped_tgt = prepare_w_tgt()
-        step(-1)
+        step(-2)
         grouped_mod = prepare_w_mod()
+        step(-1)
+        step(0)
         weights = [quantise_weight(grouped_mod, "mod"), quantise_weight(grouped_tgt, "tgt")]
-        for s in range(0, TILES + 2):
+        for s in range(1, TILES + 2):
             step(s)

@@ -48,15 +48,23 @@ def tile_ltccell_t_v_kernel(
 
         f_blk, a_blk, h_blk, g_blk, out_blk = {}, {}, {}, {}, {}
 
-        def load(blocks, rows, dtype, b, label, pieces):
-            blocks[b] = work.tile([P, BLOCK, HIDDEN], dtype, name=label, tag=label, bufs=3)
-            size = BLOCK // pieces
-            for i in range(0, BLOCK, size):
-                t = b * BLOCK + i
-                nc.sync.dma_start(out=blocks[b][:, i : i + size, :], in_=rows[:, t : t + size, :])
+        def load(stream, t, n):
+            blocks, rows, dtype, label, bufs = stream
+            if t % BLOCK == 0:
+                blocks[t // BLOCK] = work.tile([P, BLOCK, HIDDEN], dtype, name=label, tag=label, bufs=bufs)
+            i = t % BLOCK
+            nc.sync.dma_start(out=blocks[t // BLOCK][:, i : i + n, :], in_=rows[:, t : t + n, :])
+
+        f_in = (f_blk, f_rows, F32, "f_blk", 3)
+        a_in = (a_blk, a_rows, F32, "a_blk", 3)
+        h_in = (h_blk, h_rows, BF16, "h_blk", 2)
+        g_in = (g_blk, g_rows, BF16, "g_blk", 2)
 
         def row(blocks, t):
             return blocks[t // BLOCK][:, t % BLOCK, :]
+
+        def two_rows(blocks, t):
+            return blocks[t // BLOCK][:, t % BLOCK : t % BLOCK + 2, :].rearrange("p t k -> p (t k)")
 
         log_tau_4 = const.tile([P, P], BF16, name="log_tau_4")
         nc.vector.memset(log_tau_4[:], 0.0)
@@ -69,30 +77,17 @@ def tile_ltccell_t_v_kernel(
         def load_weight(label, w):
             nc.sync.dma_start(out=w_raw[label][:], in_=w[0:OUT_FEATURES, :].rearrange("(c p) k -> p c k", p=P))
 
-        def load_first(blocks, rows, dtype, label):
-            blocks[0] = work.tile([P, BLOCK, HIDDEN], dtype, name=label, tag=label, bufs=3)
-            return lambda t: nc.sync.dma_start(out=blocks[0][:, t : t + 1, :], in_=rows[:, t : t + 1, :])
-
-        load_f = load_first(f_blk, f_rows, F32, "f_blk")
-        load_a = load_first(a_blk, a_rows, F32, "a_blk")
-        load_g = load_first(g_blk, g_rows, BF16, "g_blk")
-        load_h = load_first(h_blk, h_rows, BF16, "h_blk")
-        load_f(0)
+        load(f_in, 0, 2)
         load_weight("tgt", W_tgt)
-        load_f(1)
+        load(f_in, 2, 2)
+        load(a_in, 0, 2)
         load_weight("mod", W_mod)
-        load_a(0)
-        load_g(0)
-        load_f(2)
-        load_h(0)
-        load_a(1)
-        load_g(1)
-        load_h(1)
-        load_f(3)
-        for t in range(2, BLOCK):
-            load_a(t)
-            load_g(t)
-            load_h(t)
+        load(g_in, 0, 2)
+        load(h_in, 0, 2)
+        load(f_in, 4, 4)
+        load(a_in, 2, 2)
+        load(g_in, 2, 2)
+        load(h_in, 2, 2)
 
         ident_f32 = const.tile([P, P], F32, name="ident_f32")
         make_identity(nc, ident_f32[:])
@@ -149,88 +144,107 @@ def tile_ltccell_t_v_kernel(
                 nc.vector.tensor_copy(out=pairs[:, c * P : (c + 1) * P, :], in_=flipped[:].rearrange(BY_WORD))
             return grouped
 
-        minus_f, f_sq, sign_f, v, p2, decay, a_sq, u_rows, g_signed, x7, bias_h, w1 = ({} for n in range(12))
+        minus_f, f_sq, sign_f, a_sq, u_rows, g_signed, v, p2 = ({} for n in range(8))
+        decay, x7, bias_h, w1, da, grads, grad_codes, grad_scales = ({} for n in range(8))
         nxT, vT, xT, mT, daT, acc = ({} for n in range(6))
-        da, grads, grad_codes, grad_scales = ({} for n in range(4))
+
+        def pair_tile(dtype, label):
+            return work.tile([P, 2 * HIDDEN], dtype, name=label, tag=label)
+
+        def of_pair(tiles, t):
+            return tiles[t - t % 2][:, t % 2 * HIDDEN : (t % 2 + 1) * HIDDEN]
 
         def make_minus_f(t):
-            minus_f[t] = work.tile([P, HIDDEN], F32, name="minus_f", tag="minus_f")
+            minus_f[t] = pair_tile(F32, "minus_f")
             nc.vector.tensor_scalar(
-                out=minus_f[t][:].bitcast(I32), in0=row(f_blk, t).bitcast(I32), scalar1=-(2**31), scalar2=None,
+                out=minus_f[t][:].bitcast(I32), in0=two_rows(f_blk, t).bitcast(I32), scalar1=-(2**31), scalar2=None,
                 op0=ALU.bitwise_or,
             )
 
         def make_f_sq(t):
-            f_sq[t] = work.tile([P, HIDDEN], F32, name="f_sq", tag="f_sq")
-            nc.scalar.activation(out=f_sq[t][:], in_=row(f_blk, t), func=ACT.Square, scale=SQRT_EPS)
+            f_sq[t] = pair_tile(F32, "f_sq")
+            nc.scalar.activation(out=f_sq[t][:], in_=two_rows(f_blk, t), func=ACT.Square, scale=SQRT_EPS)
 
         def make_sign(t):
-            sign_f[t] = work.tile([P, HIDDEN], BF16, name="sign_f", tag="sign_f")
-            nc.scalar.activation(out=sign_f[t][:], in_=row(f_blk, t), func=ACT.Sign)
+            sign_f[t] = pair_tile(BF16, "sign_f")
+            nc.scalar.activation(out=sign_f[t][:], in_=two_rows(f_blk, t), func=ACT.Sign)
 
-        def flip_sum(dst, terms, plain=0):
-            for j in range(PACK):
-                for n, term in enumerate(terms):
-                    last = n == len(terms) - 1
-                    nc.tensor.matmul(
-                        out=dst[:, j, :], lhsT=term[:, j * P : (j + 1) * P], rhs=ident_f32[:],
-                        is_transpose=not (last and j < plain), start=(n == 0), stop=last,
+        def make_a_sq(t):
+            a_sq[t] = pair_tile(F32, "a_sq")
+            nc.scalar.activation(out=a_sq[t][:], in_=two_rows(a_blk, t), func=ACT.Square)
+
+        def make_u(t):
+            u_rows[t] = pair_tile(F32, "u_rows")
+            nc.vector.scalar_tensor_tensor(
+                out=u_rows[t][:], in0=a_sq[t][:], scalar=1.0, in1=two_rows(g_blk, t), op0=ALU.subtract, op1=ALU.mult
+            )
+
+        def make_g_signed(t):
+            g_signed[t] = pair_tile(BF16, "g_signed")
+            nc.vector.tensor_tensor(out=g_signed[t][:], in0=two_rows(g_blk, t), in1=sign_f[t][:], op=ALU.mult)
+
+        def flip_f(half):
+            def stage(t):
+                nxT[t, half] = psum.tile([P, 2, 2, P], F32, name="nxT", tag="nxT%d" % half)
+                for jj in range(2):
+                    columns = slice((2 * half + jj) * P, (2 * half + jj + 1) * P)
+                    for i in range(2):
+                        add_transposes(
+                            nxT[t, half][:, jj, i, :],
+                            [of_pair(minus_f, t + i)[:, columns], of_pair(f_sq, t + i)[:, columns]],
+                        )
+            return stage
+
+        def make_rate(half):
+            def stage(t):
+                if half == 0:
+                    v[t] = work.tile([P, PACK, 2, P], F32, name="v", tag="v")
+                for jj in range(2):
+                    j = 2 * half + jj
+                    nc.scalar.activation(
+                        out=v[t][:, j, :, :], in_=nxT[t, half][:, jj, :, :], func=ACT.Identity,
+                        scale=minus_r0_sq[:, j : j + 1], bias=rate0[:, j : j + 1],
                     )
+            return stage
 
-        def flip_f(t):
-            nxT[t] = psum.tile([P, PACK, P], F32, name="nxT", tag="nxT", bufs=2)
-            flip_sum(nxT[t], (minus_f[t], f_sq[t]), plain=3 if t >= BLOCK - 1 else 0)
+        def make_p2(half):
+            def stage(t):
+                if half == 0:
+                    p2[t] = work.tile([P, PACK, 2, P], F32, name="p2", tag="p2", bufs=3)
+                for jj in range(2):
+                    j = 2 * half + jj
+                    nc.scalar.activation(
+                        out=p2[t][:, j, :, :], in_=nxT[t, half][:, jj, :, :], func=ACT.Square,
+                        scale=minus_r0[:, j : j + 1], bias=eps_r0_sq[:, j : j + 1],
+                    )
+            return stage
 
-        def make_rate(t):
-            v[t] = work.tile([P, PACK, P], F32, name="v", tag="v")
-            for j in range(PACK):
-                nc.scalar.activation(
-                    out=v[t][:, j, :], in_=nxT[t][:, j, :], func=ACT.Identity,
-                    scale=minus_r0_sq[:, j : j + 1], bias=rate0[:, j : j + 1],
-                )
-
-        def make_p2(t):
-            p2[t] = work.tile([P, PACK, P], F32, name="p2", tag="p2", bufs=5)
-            for j in range(PACK):
-                nc.scalar.activation(
-                    out=p2[t][:, j, :], in_=nxT[t][:, j, :], func=ACT.Square,
-                    scale=minus_r0[:, j : j + 1], bias=eps_r0_sq[:, j : j + 1],
+        def add_transposes(dst, terms):
+            for n, term in enumerate(terms):
+                nc.tensor.matmul(
+                    out=dst, lhsT=term, rhs=ident_f32[:], is_transpose=True, start=(n == 0), stop=(n == len(terms) - 1)
                 )
 
         def flip_rate(t):
             vT[t] = psum.tile([P, HIDDEN], F32, name="vT", tag="v")
             for j in range(PACK):
-                nc.tensor.transpose(vT[t][:, j * P : (j + 1) * P], v[t][:, j, :], ident_f32[:])
+                nc.tensor.transpose(vT[t][:, j * P : (j + 1) * P], v[t - t % 2][:, j, t % 2, :], ident_f32[:])
 
         def make_decay(t):
             decay[t] = work.tile([P, HIDDEN], F32, name="decay", tag="decay", bufs=3)
             nc.scalar.activation(out=decay[t][:], in_=vT[t][:], func=ACT.Exp, scale=minus_delta[:, t : t + 1])
 
-        def make_a_sq(t):
-            a_sq[t] = work.tile([P, HIDDEN], F32, name="a_sq", tag="a_sq", bufs=3)
-            nc.gpsimd.tensor_tensor(out=a_sq[t][:], in0=row(a_blk, t), in1=row(a_blk, t), op=ALU.mult)
-
-        def make_u(t):
-            u_rows[t] = work.tile([P, HIDDEN], F32, name="u_rows", tag="u_rows")
-            nc.vector.scalar_tensor_tensor(
-                out=u_rows[t][:], in0=a_sq[t][:], scalar=1.0, in1=row(g_blk, t), op0=ALU.subtract, op1=ALU.mult
-            )
-
-        def make_g_signed(t):
-            g_signed[t] = work.tile([P, HIDDEN], BF16, name="g_signed", tag="g_signed")
-            nc.vector.tensor_tensor(out=g_signed[t][:], in0=row(g_blk, t), in1=sign_f[t][:], op=ALU.mult)
-
         def make_x7(t):
             x7[t] = work.tile([P, HIDDEN], F32, name="x7", tag="x7")
             nc.vector.scalar_tensor_tensor(
-                out=x7[t][:], in0=decay[t][:], scalar=minus_delta[:, t : t + 1], in1=g_signed[t][:],
+                out=x7[t][:], in0=decay[t][:], scalar=minus_delta[:, t : t + 1], in1=of_pair(g_signed, t),
                 op0=ALU.mult, op1=ALU.mult,
             )
 
         def make_da(t):
             da[t] = work.tile([P, HIDDEN], BF16, name="da", tag="da")
             nc.vector.scalar_tensor_tensor(
-                out=da[t][:], in0=decay[t][:], scalar=1.0, in1=u_rows[t][:], op0=ALU.subtract, op1=ALU.mult
+                out=da[t][:], in0=decay[t][:], scalar=1.0, in1=of_pair(u_rows, t), op0=ALU.subtract, op1=ALU.mult
             )
 
         def flip_da(t):
@@ -241,7 +255,8 @@ def tile_ltccell_t_v_kernel(
 
         def flip_x7(t):
             xT[t] = psum.tile([P, PACK, P], F32, name="xT", tag="xT")
-            flip_sum(xT[t], (x7[t],))
+            for j in range(PACK):
+                nc.tensor.transpose(xT[t][:, j, :], x7[t][:, j * P : (j + 1) * P], ident_f32[:])
 
         def make_bias_h(t):
             bias_h[t] = work.tile([P, HIDDEN], F32, name="bias_h", tag="bias_h", bufs=3)
@@ -249,19 +264,21 @@ def tile_ltccell_t_v_kernel(
 
         def flip_m(t):
             mT[t] = psum.tile([P, PACK, P], F32, name="mT", tag="mT")
-            flip_sum(mT[t], (row(a_blk, t), bias_h[t]))
+            for j in range(PACK):
+                columns = slice(j * P, (j + 1) * P)
+                add_transposes(mT[t][:, j, :], [row(a_blk, t)[:, columns], bias_h[t][:, columns]])
 
         def make_w1(t):
             w1[t] = work.tile([P, PACK, P], F32, name="w1", tag="w1")
             for j in range(PACK):
                 nc.vector.scalar_tensor_tensor(
-                    out=w1[t][:, j, :], in0=p2[t][:, j, :], scalar=r0_sq[:, j : j + 1], in1=xT[t][:, j, :],
+                    out=w1[t][:, j, :], in0=p2[t - t % 2][:, j, t % 2, :], scalar=r0_sq[:, j : j + 1], in1=xT[t][:, j, :],
                     op0=ALU.subtract, op1=ALU.mult,
                 )
 
         def regroup_da(t):
-            grads[t] = work.tile([P, 2, P * PACK], BF16, name="grads", tag="grads", align_bytes=64)
-            nc.scalar.copy(
+            grads[t] = work.tile([P, 2, P * PACK], BF16, name="grads", tag="grads", bufs=3, align_bytes=64)
+            nc.vector.tensor_copy(
                 out=grads[t][:, 1, :].bitcast(F32).rearrange("p (t u) -> p t u", u=PAIRS),
                 in_=daT[t][:].rearrange(BY_WORD),
             )
@@ -311,48 +328,61 @@ def tile_ltccell_t_v_kernel(
             if 0 <= t < TILES:
                 stage(t)
 
-        def load_block(first_use, blocks, rows, dtype, label):
-            t = first_use + LOAD_AHEAD
-            if t % BLOCK == 0 and BLOCK <= t < TILES:
-                load(blocks, rows, dtype, t // BLOCK, label, 1)
+        def load_block(stream, t, first):
+            if t % BLOCK == 0 and first <= t < TILES:
+                load(stream, t, BLOCK)
 
         def step(s):
-            load_block(s + 3, f_blk, f_rows, F32, "f_blk")
-            load_block(s + 2, a_blk, a_rows, F32, "a_blk")
-            load_block(s + 1, g_blk, g_rows, BF16, "g_blk")
-            load_block(s + 1, h_blk, h_rows, BF16, "h_blk")
-            on(make_f_sq, s + 3)
-            on(make_decay, s + 1)
-            on(make_rate, s + 2)
-            on(make_p2, s + 2)
-            on(regroup_da, s - 1)
+            even = s % 2 == 0
+            load_block(f_in, s + 6 + LOAD_AHEAD, 2 * BLOCK)
+            load_block(a_in, s + 3 + LOAD_AHEAD, BLOCK)
+            load_block(g_in, s + 2 + LOAD_AHEAD, BLOCK)
+            load_block(h_in, s + 1 + LOAD_AHEAD, BLOCK)
             on(make_x7, s)
             on(make_da, s)
-            on(make_minus_f, s + 3)
+            if even:
+                on(make_g_signed, s + 2)
+                on(make_minus_f, s + 6)
             on(make_w1, s - 1)
-            on(make_sign, s + 2)
-            on(copy_out, s - 2)
-            on(make_bias_h, s + 1)
-            on(make_a_sq, s + 2)
-            on(make_u, s + 1)
+            on(regroup_da, s - 1)
+            on(quantise_gradients, s - 2)
             on(make_df, s - 1)
-            on(make_g_signed, s + 1)
-            on(quantise_gradients, s - 1)
-            on(flip_f, s + 3)
+            if even:
+                on(make_u, s + 2)
+            on(make_bias_h, s + 1)
+            if even:
+                on(make_p2(0), s + 2)
+            on(make_decay, s + 1)
+            if even:
+                on(copy_out, s - 4)
+                on(make_rate(1), s + 2)
+                on(make_p2(1), s + 2)
+                on(make_sign, s + 4)
+                on(make_f_sq, s + 6)
+            else:
+                on(make_a_sq, s + 3)
+                on(copy_out, s - 4)
+                on(make_rate(0), s + 3)
+                on(flip_f(1), s + 3)
+            on(multiply, s - 3)
             on(flip_x7, s)
-            on(flip_m, s)
             on(flip_da, s)
+            if even:
+                on(flip_f(0), s + 4)
+            on(flip_m, s)
             on(flip_rate, s + 2)
-            on(multiply, s - 1)
-            on(store, s - 2)
+            on(store, s - 4)
 
-        step(-3)
+        step(-6)
         make_feature_numbers()
+        step(-5)
+        step(-4)
+        step(-3)
         grouped_tgt = prepare_w_tgt()
         step(-2)
         grouped_mod = prepare_w_mod()
         step(-1)
         step(0)
         weights = [quantise_weight(grouped_mod, "mod"), quantise_weight(grouped_tgt, "tgt")]
-        for s in range(1, TILES + 2):
+        for s in range(1, TILES + 4):
             step(s)

@@ -88,6 +88,8 @@ def tile_ltccell_t_v_kernel(
         load(a_in, 2, 2)
         load(g_in, 2, 2)
         load(h_in, 2, 2)
+        for stream in (f_in, a_in, g_in, h_in):
+            load(stream, 2 * BLOCK if stream is f_in else BLOCK, BLOCK)
 
         ident_f32 = const.tile([P, P], F32, name="ident_f32")
         make_identity(nc, ident_f32[:])
@@ -172,6 +174,10 @@ def tile_ltccell_t_v_kernel(
         def make_a_sq(t):
             a_sq[t] = pair_tile(F32, "a_sq")
             nc.scalar.activation(out=a_sq[t][:], in_=two_rows(a_blk, t), func=ACT.Square)
+
+        def make_first_a_sq():
+            a_sq[0] = pair_tile(F32, "a_sq")
+            nc.gpsimd.tensor_tensor(out=a_sq[0][:], in0=two_rows(a_blk, 0), in1=two_rows(a_blk, 0), op=ALU.mult)
 
         def make_u(t):
             u_rows[t] = pair_tile(F32, "u_rows")
@@ -270,6 +276,7 @@ def tile_ltccell_t_v_kernel(
 
         def make_w1(t):
             w1[t] = work.tile([P, PACK, P], F32, name="w1", tag="w1")
+            grads[t] = work.tile([P, 2, P * PACK], BF16, name="grads", tag="grads", bufs=4, align_bytes=64)
             for j in range(PACK):
                 nc.vector.scalar_tensor_tensor(
                     out=w1[t][:, j, :], in0=p2[t - t % 2][:, j, t % 2, :], scalar=r0_sq[:, j : j + 1], in1=xT[t][:, j, :],
@@ -277,8 +284,8 @@ def tile_ltccell_t_v_kernel(
                 )
 
         def regroup_da(t):
-            grads[t] = work.tile([P, 2, P * PACK], BF16, name="grads", tag="grads", bufs=3, align_bytes=64)
-            nc.vector.tensor_copy(
+            copy = nc.vector.tensor_copy if t % 2 == 0 else nc.scalar.copy
+            copy(
                 out=grads[t][:, 1, :].bitcast(F32).rearrange("p (t u) -> p t u", u=PAIRS),
                 in_=daT[t][:].rearrange(BY_WORD),
             )
@@ -324,8 +331,8 @@ def tile_ltccell_t_v_kernel(
             elif t % BLOCK == BLOCK - 1:
                 nc.sync.dma_start(out=out_rows[:, b * BLOCK : (b + 1) * BLOCK, :], in_=out_blk[b][:])
 
-        def on(stage, t):
-            if 0 <= t < TILES:
+        def on(stage, t, first):
+            if first <= t < TILES:
                 stage(t)
 
         def load_block(stream, t, first):
@@ -334,55 +341,95 @@ def tile_ltccell_t_v_kernel(
 
         def step(s):
             even = s % 2 == 0
-            load_block(f_in, s + 6 + LOAD_AHEAD, 2 * BLOCK)
-            load_block(a_in, s + 3 + LOAD_AHEAD, BLOCK)
-            load_block(g_in, s + 2 + LOAD_AHEAD, BLOCK)
-            load_block(h_in, s + 1 + LOAD_AHEAD, BLOCK)
-            on(make_x7, s)
-            on(make_da, s)
+            load_block(f_in, s + 6 + LOAD_AHEAD, 3 * BLOCK)
+            load_block(a_in, s + 3 + LOAD_AHEAD, 2 * BLOCK)
+            load_block(g_in, s + 2 + LOAD_AHEAD, 2 * BLOCK)
+            load_block(h_in, s + 1 + LOAD_AHEAD, 2 * BLOCK)
+            on(quantise_gradients, s - 3, 0)
+            on(make_x7, s, 2)
+            on(make_da, s, 2)
             if even:
-                on(make_g_signed, s + 2)
-                on(make_minus_f, s + 6)
-            on(make_w1, s - 1)
-            on(regroup_da, s - 1)
-            on(quantise_gradients, s - 2)
-            on(make_df, s - 1)
+                on(make_g_signed, s + 2, 4)
+                on(make_minus_f, s + 6, 6)
+            on(make_w1, s - 1, 1)
+            if not even:
+                on(regroup_da, s - 1, 1)
+            on(make_df, s - 1, 1)
             if even:
-                on(make_u, s + 2)
-            on(make_bias_h, s + 1)
+                on(make_u, s + 2, 4)
+            on(make_bias_h, s + 1, 4)
             if even:
-                on(make_p2(0), s + 2)
-            on(make_decay, s + 1)
+                on(make_p2(0), s + 2, 4)
+                on(regroup_da, s - 1, 1)
+            on(make_decay, s + 1, 2)
             if even:
-                on(copy_out, s - 4)
-                on(make_rate(1), s + 2)
-                on(make_p2(1), s + 2)
-                on(make_sign, s + 4)
-                on(make_f_sq, s + 6)
+                on(copy_out, s - 4, 0)
+                on(make_rate(1), s + 2, 4)
+                on(make_p2(1), s + 2, 4)
+                on(make_sign, s + 4, 4)
+                on(make_f_sq, s + 6, 6)
             else:
-                on(make_a_sq, s + 3)
-                on(copy_out, s - 4)
-                on(make_rate(0), s + 3)
-                on(flip_f(1), s + 3)
-            on(multiply, s - 3)
-            on(flip_x7, s)
-            on(flip_da, s)
+                on(make_a_sq, s + 3, 4)
+                on(copy_out, s - 4, 0)
+                on(make_rate(0), s + 3, 4)
+                on(flip_f(1), s + 3, 4)
+            on(multiply, s - 3, 0)
+            on(flip_x7, s, 1)
+            on(flip_da, s, 1)
             if even:
-                on(flip_f(0), s + 4)
-            on(flip_m, s)
-            on(flip_rate, s + 2)
-            on(store, s - 4)
+                on(flip_f(0), s + 4, 4)
+            on(flip_m, s, 1)
+            on(flip_rate, s + 2, 3)
+            on(store, s - 4, 0)
 
-        step(-6)
+        make_f_sq(0)
+        make_minus_f(0)
         make_feature_numbers()
-        step(-5)
-        step(-4)
-        step(-3)
+        make_sign(0)
+        make_f_sq(2)
+        make_minus_f(2)
+        for half in range(2):
+            flip_f(half)(0)
         grouped_tgt = prepare_w_tgt()
-        step(-2)
+        for half in range(2):
+            make_rate(half)(0)
+        make_first_a_sq()
+        make_bias_h(0)
+        make_g_signed(0)
+        make_u(0)
+        flip_rate(0)
+        for half in range(2):
+            make_p2(half)(0)
+        flip_f(0)(2)
+        make_decay(0)
+        flip_rate(1)
+        flip_f(1)(2)
+        make_sign(2)
+        make_rate(0)(2)
+        make_decay(1)
+        make_p2(0)(2)
+        make_rate(1)(2)
+        make_p2(1)(2)
+        make_a_sq(2)
+        make_f_sq(4)
+        make_x7(0)
+        make_da(0)
+        make_minus_f(4)
+        make_x7(1)
+        make_da(1)
+        make_g_signed(2)
+        flip_x7(0)
+        flip_da(0)
+        flip_m(0)
+        flip_rate(2)
+        for t in range(1, 4):
+            make_bias_h(t)
+        make_w1(0)
+        regroup_da(0)
+        make_df(0)
+        make_u(2)
         grouped_mod = prepare_w_mod()
-        step(-1)
-        step(0)
-        weights = [quantise_weight(grouped_mod, "mod"), quantise_weight(grouped_tgt, "tgt")]
-        for s in range(1, TILES + 4):
+        for s in range(0, TILES + 4):
+            if s == 3:
+                weights = [quantise_weight(grouped_mod, "mod"), quantise_weight(grouped_tgt, "tgt")]
             step(s)

@@ -125,26 +125,41 @@ def tile_ltccell_t_v_kernel(
             )
             return codes, scales
 
-        def prepare_w_mod():
-            grouped = const.tile([P, OUT_FEATURES, PACK], BF16, name="w_grouped_mod", align_bytes=64)
+        flipped_mod, flipped_tgt = {}, {}
+        grouped_mod = const.tile([P, OUT_FEATURES, PACK], BF16, name="grouped_mod", align_bytes=64)
+        grouped_tgt = const.tile([P, OUT_FEATURES, PACK], BF16, name="grouped_tgt", align_bytes=64)
+
+        def flip_w_mod():
             for c in range(OUT_FEATURES // P):
-                flipped = psum.tile([P, PACK, P], BF16, name="w_flipped", tag="acc", bufs=2)
+                if c % 2 == 0:
+                    flipped_mod[c] = psum.tile([P, 2, PACK, P], BF16, name="flipped_mod", tag="acc", bufs=2)
                 for j in range(PACK):
-                    nc.tensor.transpose(flipped[:, j, :], w_raw["mod"][:, c, j * P : (j + 1) * P], ident_bf16[:])
-                nc.vector.tensor_copy(out=grouped[:, c * P : (c + 1) * P, :], in_=flipped[:].rearrange(BY_WORD))
-            return grouped
+                    nc.tensor.transpose(
+                        flipped_mod[c - c % 2][:, c % 2, j, :], w_raw["mod"][:, c, j * P : (j + 1) * P], ident_bf16[:]
+                    )
+
+        def copy_w_mod():
+            for c in range(0, OUT_FEATURES // P, 2):
+                nc.scalar.copy(
+                    out=grouped_mod[:, c * P : (c + 2) * P, :].rearrange("p (c t) j -> p c t j", c=2),
+                    in_=flipped_mod[c][:].rearrange("p c j t -> p c t j"),
+                )
 
         def prepare_w_tgt():
-            grouped = const.tile([P, OUT_FEATURES, PACK], BF16, name="w_grouped_tgt", align_bytes=64)
             words = w_raw["tgt"][:].rearrange("p c k -> p (c k)").bitcast(F32)
-            pairs = grouped[:].rearrange("p i j -> p (i j)").bitcast(F32).rearrange("p (i u) -> p i u", u=PAIRS)
+            pairs = grouped_tgt[:].rearrange("p i j -> p (i j)").bitcast(F32).rearrange("p (c t u) -> p c t u", t=P, u=PAIRS)
             for c in range(OUT_FEATURES // P):
-                flipped = psum.tile([P, PAIRS, P], F32, name="w_flipped_words", tag="acc", bufs=2)
+                if c % 2 == 0:
+                    flipped_tgt[c] = psum.tile([P, 2, PAIRS, P], F32, name="flipped_tgt", tag="acc", bufs=2)
                 for u in range(PAIRS):
                     first = c * HIDDEN // 2 + u * P
-                    nc.tensor.transpose(flipped[:, u, :], words[:, first : first + P], ident_f32[:])
-                nc.vector.tensor_copy(out=pairs[:, c * P : (c + 1) * P, :], in_=flipped[:].rearrange(BY_WORD))
-            return grouped
+                    nc.tensor.transpose(
+                        flipped_tgt[c - c % 2][:, c % 2, u, :], words[:, first : first + P], ident_f32[:]
+                    )
+            for c in range(0, OUT_FEATURES // P, 2):
+                nc.vector.tensor_copy(
+                    out=pairs[:, c : c + 2, :, :], in_=flipped_tgt[c][:].rearrange("p c u t -> p c t u")
+                )
 
         minus_f, f_sq, sign_f, a_sq, u_rows, g_signed, v, p2 = ({} for n in range(8))
         decay, x7, bias_h, w1, da, grads, grad_codes, grad_scales = ({} for n in range(8))
@@ -205,7 +220,7 @@ def tile_ltccell_t_v_kernel(
             def stage(t):
                 if half == 0:
                     v[t] = work.tile([P, PACK, 2, P], F32, name="v", tag="v")
-                for jj in range(2):
+                for jj in reversed(range(2)):
                     j = 2 * half + jj
                     nc.scalar.activation(
                         out=v[t][:, j, :, :], in_=nxT[t, half][:, jj, :, :], func=ACT.Identity,
@@ -233,7 +248,7 @@ def tile_ltccell_t_v_kernel(
 
         def flip_rate(t):
             vT[t] = psum.tile([P, HIDDEN], F32, name="vT", tag="v")
-            for j in range(PACK):
+            for j in (2, 3, 0, 1):
                 nc.tensor.transpose(vT[t][:, j * P : (j + 1) * P], v[t - t % 2][:, j, t % 2, :], ident_f32[:])
 
         def make_decay(t):
@@ -277,14 +292,14 @@ def tile_ltccell_t_v_kernel(
         def make_w1(t):
             w1[t] = work.tile([P, PACK, P], F32, name="w1", tag="w1")
             grads[t] = work.tile([P, 2, P * PACK], BF16, name="grads", tag="grads", bufs=4, align_bytes=64)
-            for j in range(PACK):
+            for j in reversed(range(PACK)):
                 nc.vector.scalar_tensor_tensor(
                     out=w1[t][:, j, :], in0=p2[t - t % 2][:, j, t % 2, :], scalar=r0_sq[:, j : j + 1], in1=xT[t][:, j, :],
                     op0=ALU.subtract, op1=ALU.mult,
                 )
 
         def regroup_da(t):
-            copy = nc.vector.tensor_copy if t % 2 == 0 else nc.scalar.copy
+            copy = nc.vector.tensor_copy if t % 4 == 0 else nc.scalar.copy
             copy(
                 out=grads[t][:, 1, :].bitcast(F32).rearrange("p (t u) -> p t u", u=PAIRS),
                 in_=daT[t][:].rearrange(BY_WORD),
@@ -352,7 +367,7 @@ def tile_ltccell_t_v_kernel(
                 on(make_g_signed, s + 2, 4)
                 on(make_minus_f, s + 6, 6)
             on(make_w1, s - 1, 1)
-            if not even:
+            if s % 4 == 1:
                 on(regroup_da, s - 1, 1)
             on(make_df, s - 1, 1)
             if even:
@@ -360,6 +375,7 @@ def tile_ltccell_t_v_kernel(
             on(make_bias_h, s + 1, 4)
             if even:
                 on(make_p2(0), s + 2, 4)
+            if s % 4 != 1:
                 on(regroup_da, s - 1, 1)
             on(make_decay, s + 1, 2)
             if even:
@@ -390,7 +406,7 @@ def tile_ltccell_t_v_kernel(
         make_minus_f(2)
         for half in range(2):
             flip_f(half)(0)
-        grouped_tgt = prepare_w_tgt()
+        prepare_w_tgt()
         for half in range(2):
             make_rate(half)(0)
         make_first_a_sq()
@@ -428,8 +444,10 @@ def tile_ltccell_t_v_kernel(
         regroup_da(0)
         make_df(0)
         make_u(2)
-        grouped_mod = prepare_w_mod()
+        flip_w_mod()
         for s in range(0, TILES + 4):
+            if s == 2:
+                copy_w_mod()
             if s == 3:
                 weights = [quantise_weight(grouped_mod, "mod"), quantise_weight(grouped_tgt, "tgt")]
             step(s)

@@ -27,6 +27,7 @@ FLOPS = 2 * TOKENS * OUT_FEATURES * 2 * HIDDEN
 BYTES = TOKENS * HIDDEN * (2 + 2 + 4 + 4) + TOKENS * OUT_FEATURES * 4 + 2 * OUT_FEATURES * HIDDEN * 2
 
 BY_WORD = "p j t -> p t j"
+BY_FOURS = "p j (c i) -> p c j i"
 
 
 def tile_ltccell_t_v_kernel(
@@ -77,7 +78,8 @@ def tile_ltccell_t_v_kernel(
         def load_weight(label, w):
             nc.sync.dma_start(out=w_raw[label][:], in_=w[0:OUT_FEATURES, :].rearrange("(c p) k -> p c k", p=P))
 
-        load(f_in, 0, 2)
+        load(f_in, 0, 1)
+        load(f_in, 1, 1)
         load_weight("tgt", W_tgt)
         load(f_in, 2, 2)
         load(a_in, 0, 2)
@@ -178,9 +180,14 @@ def tile_ltccell_t_v_kernel(
                 op0=ALU.bitwise_or,
             )
 
-        def make_f_sq(t):
+        def make_f_sq(t, parts=1):
             f_sq[t] = pair_tile(F32, "f_sq")
-            nc.scalar.activation(out=f_sq[t][:], in_=two_rows(f_blk, t), func=ACT.Square, scale=SQRT_EPS)
+            size = 2 * HIDDEN // parts
+            for i in range(parts):
+                columns = slice(i * size, (i + 1) * size)
+                nc.scalar.activation(
+                    out=f_sq[t][:, columns], in_=two_rows(f_blk, t)[:, columns], func=ACT.Square, scale=SQRT_EPS
+                )
 
         def make_sign(t):
             sign_f[t] = pair_tile(BF16, "sign_f")
@@ -299,7 +306,7 @@ def tile_ltccell_t_v_kernel(
                 )
 
         def regroup_da(t):
-            copy = nc.vector.tensor_copy if t % 4 == 0 else nc.scalar.copy
+            copy = nc.vector.tensor_copy if t % 2 == 0 else nc.scalar.copy
             copy(
                 out=grads[t][:, 1, :].bitcast(F32).rearrange("p (t u) -> p t u", u=PAIRS),
                 in_=daT[t][:].rearrange(BY_WORD),
@@ -307,8 +314,8 @@ def tile_ltccell_t_v_kernel(
 
         def make_df(t):
             nc.vector.tensor_tensor(
-                out=grads[t][:, 0, :].rearrange("p (t j) -> p t j", j=PACK), in0=mT[t][:].rearrange(BY_WORD),
-                in1=w1[t][:].rearrange(BY_WORD), op=ALU.mult,
+                out=grads[t][:, 0, :].rearrange("p (c i j) -> p c j i", i=4, j=PACK),
+                in0=mT[t][:].rearrange(BY_FOURS, i=4), in1=w1[t][:].rearrange(BY_FOURS, i=4), op=ALU.mult,
             )
 
         def quantise_gradients(t):
@@ -367,7 +374,7 @@ def tile_ltccell_t_v_kernel(
                 on(make_g_signed, s + 2, 4)
                 on(make_minus_f, s + 6, 6)
             on(make_w1, s - 1, 1)
-            if s % 4 == 1:
+            if not even:
                 on(regroup_da, s - 1, 1)
             on(make_df, s - 1, 1)
             if even:
@@ -375,7 +382,7 @@ def tile_ltccell_t_v_kernel(
             on(make_bias_h, s + 1, 4)
             if even:
                 on(make_p2(0), s + 2, 4)
-            if s % 4 != 1:
+            if even:
                 on(regroup_da, s - 1, 1)
             on(make_decay, s + 1, 2)
             if even:
@@ -398,7 +405,7 @@ def tile_ltccell_t_v_kernel(
             on(flip_rate, s + 2, 3)
             on(store, s - 4, 0)
 
-        make_f_sq(0)
+        make_f_sq(0, parts=2)
         make_minus_f(0)
         make_feature_numbers()
         make_sign(0)

from contextlib import ExitStack

import concourse.mybir as mybir
from concourse.masks import make_identity

F32 = mybir.dt.float32
BF16 = mybir.dt.bfloat16
I32 = mybir.dt.int32
U32 = mybir.dt.uint32
U8 = mybir.dt.uint8
E4M3_X4 = mybir.dt.float8_e4m3fn_x4
E5M2_X4 = mybir.dt.float8_e5m2_x4
ACT = mybir.ActivationFunctionType
ALU = mybir.AluOpType

P = 128
TOKENS, HIDDEN, OUT_FEATURES = 4096, 512, 512
EPS = 1e-6
SQRT_EPS = 1e-3
TILES = TOKENS // P
PACK = HIDDEN // P
PAIRS = HIDDEN // 2 // P
BLOCK = 4
LOAD_AHEAD = 4

FLOPS = 2 * TOKENS * OUT_FEATURES * 2 * HIDDEN
BYTES = TOKENS * HIDDEN * (2 + 2 + 4 + 4) + TOKENS * OUT_FEATURES * 4 + 2 * OUT_FEATURES * HIDDEN * 2

BY_WORD = "p j t -> p t j"
BY_FOURS = "p j (c i) -> p c j i"


def tile_ltccell_t_v_kernel(
    tc, x, h, time_delta, W_mod, b_mod, W_tgt, b_tgt, log_tau, bias, f, a, grad_out, out
):
    nc = tc.nc
    by_tile = "(p t) k -> p t k"
    f_rows = f.rearrange(by_tile, t=TILES)
    a_rows = a.rearrange(by_tile, t=TILES)
    h_rows = h.rearrange(by_tile, t=TILES)
    g_rows = grad_out.rearrange(by_tile, t=TILES)
    out_rows = out.rearrange(by_tile, t=TILES)

    with ExitStack() as stack:
        stack.enter_context(tc.manual_schedule())
        const = stack.enter_context(tc.tile_pool(name="const", bufs=1))
        work = stack.enter_context(tc.tile_pool(name="work", bufs=2))
        psum = stack.enter_context(tc.psum_pool(name="psum", bufs=1))

        f_blk, a_blk, h_blk, g_blk, out_blk = {}, {}, {}, {}, {}

        def load(stream, t, n):
            blocks, rows, dtype, label, bufs = stream
            if t % BLOCK == 0:
                blocks[t // BLOCK] = work.tile([P, BLOCK, HIDDEN], dtype, name=label, tag=label, bufs=bufs)
            i = t % BLOCK
            nc.sync.dma_start(out=blocks[t // BLOCK][:, i : i + n, :], in_=rows[:, t : t + n, :])

        f_in = (f_blk, f_rows, F32, "f_blk", 3)
        a_in = (a_blk, a_rows, F32, "a_blk", 3)
        h_in = (h_blk, h_rows, BF16, "h_blk", 2)
        g_in = (g_blk, g_rows, BF16, "g_blk", 2)

        def row(blocks, t):
            return blocks[t // BLOCK][:, t % BLOCK, :]

        def two_rows(blocks, t):
            return blocks[t // BLOCK][:, t % BLOCK : t % BLOCK + 2, :].rearrange("p t k -> p (t k)")

        log_tau_4 = const.tile([P, P], BF16, name="log_tau_4")
        nc.vector.memset(log_tau_4[:], 0.0)
        nc.sync.dma_start(out=log_tau_4[0:PACK, :], in_=log_tau.rearrange("(j p) -> j p", p=P))
        delta = const.tile([P, TILES], BF16, name="delta")
        nc.scalar.dma_start(out=delta[:], in_=time_delta.rearrange("(p t) o -> p (t o)", t=TILES))
        bias_rows = const.tile([P, HIDDEN], BF16, name="bias_rows")
        w_raw = {label: const.tile([P, PACK, HIDDEN], BF16, name="w_raw_" + label) for label in ("mod", "tgt")}

        def load_weight(label, w):
            nc.sync.dma_start(out=w_raw[label][:], in_=w[0:OUT_FEATURES, :].rearrange("(c p) k -> p c k", p=P))

        load(f_in, 0, 1)
        load(f_in, 1, 1)
        load_weight("tgt", W_tgt)
        load(f_in, 2, 2)
        load(a_in, 0, 2)
        load_weight("mod", W_mod)
        load(g_in, 0, 2)
        load(h_in, 0, 2)
        load(f_in, 4, 4)
        load(a_in, 2, 2)
        load(g_in, 2, 2)
        load(h_in, 2, 2)
        for stream in (f_in, a_in, g_in, h_in):
            load(stream, 2 * BLOCK if stream is f_in else BLOCK, BLOCK)

        ident_f32 = const.tile([P, P], F32, name="ident_f32")
        make_identity(nc, ident_f32[:])
        ident_bf16 = const.tile([P, P], BF16, name="ident_bf16")
        make_identity(nc, ident_bf16[:])
        nc.gpsimd.dma_start(out=bias_rows[:], in_=bias.partition_broadcast(P))

        clamped, tau, den, rate0, r0, minus_r0, r0_sq, minus_r0_sq, eps_r0_sq = (
            const.tile([P, PACK], F32, name="feature_%d" % n) for n in range(9)
        )
        minus_delta = const.tile([P, TILES], F32, name="minus_delta")

        lt_T = psum.tile([P, P], BF16, name="lt_T", tag="v")
        nc.tensor.transpose(lt_T[:], log_tau_4[:], ident_bf16[:])

        def make_feature_numbers():
            nc.vector.tensor_scalar(out=clamped[:], in0=lt_T[:, 0:PACK], scalar1=80.0, scalar2=None, op0=ALU.min)
            nc.scalar.activation(out=tau[:], in_=clamped[:], func=ACT.Exp)
            nc.vector.tensor_scalar(out=den[:], in0=tau[:], scalar1=EPS, scalar2=None, op0=ALU.add)
            nc.vector.reciprocal(out=rate0[:], in_=den[:])
            nc.vector.tensor_tensor(out=r0[:], in0=tau[:], in1=rate0[:], op=ALU.mult)
            nc.vector.tensor_scalar(out=minus_r0[:], in0=r0[:], scalar1=-1.0, scalar2=None, op0=ALU.mult)
            nc.vector.tensor_tensor(out=r0_sq[:], in0=r0[:], in1=r0[:], op=ALU.mult)
            nc.vector.tensor_scalar(out=minus_r0_sq[:], in0=r0_sq[:], scalar1=-1.0, scalar2=None, op0=ALU.mult)
            nc.vector.tensor_scalar(out=eps_r0_sq[:], in0=r0_sq[:], scalar1=EPS, scalar2=None, op0=ALU.mult)
            nc.vector.tensor_scalar(out=minus_delta[:], in0=delta[:], scalar1=-1.0, scalar2=None, op0=ALU.mult)

        def quantise_weight(grouped, label):
            codes = const.tile([P, OUT_FEATURES], U32, name="codes_" + label, align_bytes=64)
            scales = const.tile([P, OUT_FEATURES], U8, name="scales_" + label, align_bytes=64)
            nc.vector.quantize_mx(
                out=codes[:].bitcast(E4M3_X4), scales=scales[:], in_=grouped[:].rearrange("p i j -> p (i j)")
            )
            return codes, scales

        flipped_mod, flipped_tgt = {}, {}
        grouped_mod = const.tile([P, OUT_FEATURES, PACK], BF16, name="grouped_mod", align_bytes=64)
        grouped_tgt = const.tile([P, OUT_FEATURES, PACK], BF16, name="grouped_tgt", align_bytes=64)

        def flip_w_mod():
            for c in range(OUT_FEATURES // P):
                if c % 2 == 0:
                    flipped_mod[c] = psum.tile([P, 2, PACK, P], BF16, name="flipped_mod", tag="acc", bufs=2)
                for j in range(PACK):
                    nc.tensor.transpose(
                        flipped_mod[c - c % 2][:, c % 2, j, :], w_raw["mod"][:, c, j * P : (j + 1) * P], ident_bf16[:]
                    )

        def copy_w_mod():
            for c in range(0, OUT_FEATURES // P, 2):
                nc.scalar.copy(
                    out=grouped_mod[:, c * P : (c + 2) * P, :].rearrange("p (c t) j -> p c t j", c=2),
                    in_=flipped_mod[c][:].rearrange("p c j t -> p c t j"),
                )

        def prepare_w_tgt():
            words = w_raw["tgt"][:].rearrange("p c k -> p (c k)").bitcast(F32)
            pairs = grouped_tgt[:].rearrange("p i j -> p (i j)").bitcast(F32).rearrange("p (c t u) -> p c t u", t=P, u=PAIRS)
            for c in range(OUT_FEATURES // P):
                if c % 2 == 0:
                    flipped_tgt[c] = psum.tile([P, 2, PAIRS, P], F32, name="flipped_tgt", tag="acc", bufs=2)
                for u in range(PAIRS):
                    first = c * HIDDEN // 2 + u * P
                    nc.tensor.transpose(
                        flipped_tgt[c - c % 2][:, c % 2, u, :], words[:, first : first + P], ident_f32[:]
                    )
            for c in range(0, OUT_FEATURES // P, 2):
                nc.vector.tensor_copy(
                    out=pairs[:, c : c + 2, :, :], in_=flipped_tgt[c][:].rearrange("p c u t -> p c t u")
                )

        minus_f, f_sq, sign_f, a_sq, u_rows, g_signed, v, p2 = ({} for n in range(8))
        decay, x7, bias_h, w1, da, grads, grad_codes, grad_scales = ({} for n in range(8))
        nxT, vT, xT, mT, daT, acc = ({} for n in range(6))

        def pair_tile(dtype, label):
            return work.tile([P, 2 * HIDDEN], dtype, name=label, tag=label)

        def of_pair(tiles, t):
            return tiles[t - t % 2][:, t % 2 * HIDDEN : (t % 2 + 1) * HIDDEN]

        def make_minus_f(t):
            minus_f[t] = pair_tile(F32, "minus_f")
            nc.vector.tensor_scalar(
                out=minus_f[t][:].bitcast(I32), in0=two_rows(f_blk, t).bitcast(I32), scalar1=-(2**31), scalar2=None,
                op0=ALU.bitwise_or,
            )

        def make_f_sq(t, parts=1):
            f_sq[t] = pair_tile(F32, "f_sq")
            size = 2 * HIDDEN // parts
            for i in range(parts):
                columns = slice(i * size, (i + 1) * size)
                nc.scalar.activation(
                    out=f_sq[t][:, columns], in_=two_rows(f_blk, t)[:, columns], func=ACT.Square, scale=SQRT_EPS
                )

        def make_sign(t):
            sign_f[t] = pair_tile(BF16, "sign_f")
            nc.scalar.activation(out=sign_f[t][:], in_=two_rows(f_blk, t), func=ACT.Sign)

        def make_a_sq(t):
            a_sq[t] = pair_tile(F32, "a_sq")
            nc.scalar.activation(out=a_sq[t][:], in_=two_rows(a_blk, t), func=ACT.Square)

        def make_first_a_sq():
            a_sq[0] = pair_tile(F32, "a_sq")
            nc.gpsimd.tensor_tensor(out=a_sq[0][:], in0=two_rows(a_blk, 0), in1=two_rows(a_blk, 0), op=ALU.mult)

        def make_u(t):
            u_rows[t] = pair_tile(F32, "u_rows")
            nc.vector.scalar_tensor_tensor(
                out=u_rows[t][:], in0=a_sq[t][:], scalar=1.0, in1=two_rows(g_blk, t), op0=ALU.subtract, op1=ALU.mult
            )

        def make_g_signed(t):
            g_signed[t] = pair_tile(BF16, "g_signed")
            nc.vector.tensor_tensor(out=g_signed[t][:], in0=two_rows(g_blk, t), in1=sign_f[t][:], op=ALU.mult)

        def flip_f(half):
            def stage(t):
                nxT[t, half] = psum.tile([P, 2, 2, P], F32, name="nxT", tag="nxT%d" % half)
                for jj in range(2):
                    columns = slice((2 * half + jj) * P, (2 * half + jj + 1) * P)
                    for i in range(2):
                        add_transposes(
                            nxT[t, half][:, jj, i, :],
                            [of_pair(minus_f, t + i)[:, columns], of_pair(f_sq, t + i)[:, columns]],
                        )
            return stage

        def make_rate(half):
            def stage(t):
                if half == 0:
                    v[t] = work.tile([P, PACK, 2, P], F32, name="v", tag="v")
                for jj in reversed(range(2)):
                    j = 2 * half + jj
                    nc.scalar.activation(
                        out=v[t][:, j, :, :], in_=nxT[t, half][:, jj, :, :], func=ACT.Identity,
                        scale=minus_r0_sq[:, j : j + 1], bias=rate0[:, j : j + 1],
                    )
            return stage

        def make_p2(half):
            def stage(t):
                if half == 0:
                    p2[t] = work.tile([P, PACK, 2, P], F32, name="p2", tag="p2", bufs=3)
                for jj in range(2):
                    j = 2 * half + jj
                    nc.scalar.activation(
                        out=p2[t][:, j, :, :], in_=nxT[t, half][:, jj, :, :], func=ACT.Square,
                        scale=minus_r0[:, j : j + 1], bias=eps_r0_sq[:, j : j + 1],
                    )
            return stage

        def add_transposes(dst, terms):
            for n, term in enumerate(terms):
                nc.tensor.matmul(
                    out=dst, lhsT=term, rhs=ident_f32[:], is_transpose=True, start=(n == 0), stop=(n == len(terms) - 1)
                )

        def flip_rate(t):
            vT[t] = psum.tile([P, HIDDEN], F32, name="vT", tag="v")
            for j in (2, 3, 0, 1):
                nc.tensor.transpose(vT[t][:, j * P : (j + 1) * P], v[t - t % 2][:, j, t % 2, :], ident_f32[:])

        def make_decay(t):
            decay[t] = work.tile([P, HIDDEN], F32, name="decay", tag="decay", bufs=3)
            nc.scalar.activation(out=decay[t][:], in_=vT[t][:], func=ACT.Exp, scale=minus_delta[:, t : t + 1])

        def make_x7(t):
            x7[t] = work.tile([P, HIDDEN], F32, name="x7", tag="x7")
            nc.vector.scalar_tensor_tensor(
                out=x7[t][:], in0=decay[t][:], scalar=minus_delta[:, t : t + 1], in1=of_pair(g_signed, t),
                op0=ALU.mult, op1=ALU.mult,
            )

        def make_da(t):
            da[t] = work.tile([P, HIDDEN], BF16, name="da", tag="da")
            nc.vector.scalar_tensor_tensor(
                out=da[t][:], in0=decay[t][:], scalar=1.0, in1=of_pair(u_rows, t), op0=ALU.subtract, op1=ALU.mult
            )

        def flip_da(t):
            daT[t] = psum.tile([P, PAIRS, P], F32, name="daT", tag="daT")
            words = da[t][:].bitcast(F32)
            for u in range(PAIRS):
                nc.tensor.transpose(daT[t][:, u, :], words[:, u * P : (u + 1) * P], ident_f32[:])

        def flip_x7(t):
            xT[t] = psum.tile([P, PACK, P], F32, name="xT", tag="xT")
            for j in range(PACK):
                nc.tensor.transpose(xT[t][:, j, :], x7[t][:, j * P : (j + 1) * P], ident_f32[:])

        def make_bias_h(t):
            bias_h[t] = work.tile([P, HIDDEN], F32, name="bias_h", tag="bias_h", bufs=3)
            nc.gpsimd.tensor_tensor(out=bias_h[t][:], in0=bias_rows[:], in1=row(h_blk, t), op=ALU.subtract)

        def flip_m(t):
            mT[t] = psum.tile([P, PACK, P], F32, name="mT", tag="mT")
            for j in range(PACK):
                columns = slice(j * P, (j + 1) * P)
                add_transposes(mT[t][:, j, :], [row(a_blk, t)[:, columns], bias_h[t][:, columns]])

        def make_w1(t):
            w1[t] = work.tile([P, PACK, P], F32, name="w1", tag="w1")
            grads[t] = work.tile([P, 2, P * PACK], BF16, name="grads", tag="grads", bufs=4, align_bytes=64)
            for j in reversed(range(PACK)):
                nc.vector.scalar_tensor_tensor(
                    out=w1[t][:, j, :], in0=p2[t - t % 2][:, j, t % 2, :], scalar=r0_sq[:, j : j + 1], in1=xT[t][:, j, :],
                    op0=ALU.subtract, op1=ALU.mult,
                )

        def regroup_da(t):
            copy = nc.vector.tensor_copy if t % 2 == 0 else nc.scalar.copy
            copy(
                out=grads[t][:, 1, :].bitcast(F32).rearrange("p (t u) -> p t u", u=PAIRS),
                in_=daT[t][:].rearrange(BY_WORD),
            )

        def make_df(t):
            nc.vector.tensor_tensor(
                out=grads[t][:, 0, :].rearrange("p (c i j) -> p c j i", i=4, j=PACK),
                in0=mT[t][:].rearrange(BY_FOURS, i=4), in1=w1[t][:].rearrange(BY_FOURS, i=4), op=ALU.mult,
            )

        def quantise_gradients(t):
            grad_codes[t] = work.tile([P, 2 * P], U32, name="grad_codes", tag="grad_codes", align_bytes=64)
            grad_scales[t] = work.tile([P, 2 * P], U8, name="grad_scales", tag="grad_scales", align_bytes=64)
            nc.vector.quantize_mx(
                out=grad_codes[t][:].bitcast(E5M2_X4), scales=grad_scales[t][:],
                in_=grads[t][:].rearrange("p s k -> p (s k)"),
            )

        def multiply(t):
            acc[t] = psum.tile([P, OUT_FEATURES], F32, name="acc", tag="acc", bufs=2)
            for n, (codes, scales) in enumerate(weights):
                tokens = slice(n * P, (n + 1) * P)
                nc.tensor.matmul_mx(
                    out=acc[t][:],
                    lhsT=grad_codes[t][:, tokens].bitcast(E5M2_X4),
                    lhsT_scale=grad_scales[t][:, tokens],
                    rhs=codes[:].bitcast(E4M3_X4),
                    rhs_scale=scales[:],
                    start=(n == 0),
                    stop=(n == 1),
                )

        def copy_out(t):
            b = t // BLOCK
            if t % BLOCK == 0:
                out_blk[b] = work.tile([P, BLOCK, OUT_FEATURES], F32, name="out_blk", tag="out_blk")
            nc.scalar.copy(out=row(out_blk, t), in_=acc[t][:])

        def store(t):
            b = t // BLOCK
            if b == TILES // BLOCK - 1:
                nc.sync.dma_start(out=out_rows[:, t : t + 1, :], in_=out_blk[b][:, t % BLOCK : t % BLOCK + 1, :])
            elif t % BLOCK == BLOCK - 1:
                nc.sync.dma_start(out=out_rows[:, b * BLOCK : (b + 1) * BLOCK, :], in_=out_blk[b][:])

        def on(stage, t, first):
            if first <= t < TILES:
                stage(t)

        def load_block(stream, t, first):
            if t % BLOCK == 0 and first <= t < TILES:
                load(stream, t, BLOCK)

        def step(s):
            even = s % 2 == 0
            load_block(f_in, s + 6 + LOAD_AHEAD, 3 * BLOCK)
            load_block(a_in, s + 3 + LOAD_AHEAD, 2 * BLOCK)
            load_block(g_in, s + 2 + LOAD_AHEAD, 2 * BLOCK)
            load_block(h_in, s + 1 + LOAD_AHEAD, 2 * BLOCK)
            on(quantise_gradients, s - 3, 0)
            on(make_x7, s, 2)
            on(make_da, s, 2)
            if even:
                on(make_g_signed, s + 2, 4)
                on(make_minus_f, s + 6, 6)
            on(make_w1, s - 1, 1)
            if not even:
                on(regroup_da, s - 1, 1)
            on(make_df, s - 1, 1)
            if even:
                on(make_u, s + 2, 4)
            on(make_bias_h, s + 1, 4)
            if even:
                on(make_p2(0), s + 2, 4)
            if even:
                on(regroup_da, s - 1, 1)
            on(make_decay, s + 1, 2)
            if even:
                on(copy_out, s - 4, 0)
                on(make_rate(1), s + 2, 4)
                on(make_p2(1), s + 2, 4)
                on(make_sign, s + 4, 4)
                on(make_f_sq, s + 6, 6)
            else:
                on(make_a_sq, s + 3, 4)
                on(copy_out, s - 4, 0)
                on(make_rate(0), s + 3, 4)
                on(flip_f(1), s + 3, 4)
            on(multiply, s - 3, 0)
            on(flip_x7, s, 1)
            on(flip_da, s, 1)
            if even:
                on(flip_f(0), s + 4, 4)
            on(flip_m, s, 1)
            on(flip_rate, s + 2, 3)
            on(store, s - 4, 0)

        make_f_sq(0, parts=2)
        make_minus_f(0)
        make_feature_numbers()
        make_sign(0)
        make_f_sq(2)
        make_minus_f(2)
        for half in range(2):
            flip_f(half)(0)
        prepare_w_tgt()
        for half in range(2):
            make_rate(half)(0)
        make_first_a_sq()
        make_bias_h(0)
        make_g_signed(0)
        make_u(0)
        flip_rate(0)
        for half in range(2):
            make_p2(half)(0)
        flip_f(0)(2)
        make_decay(0)
        flip_rate(1)
        flip_f(1)(2)
        make_sign(2)
        make_rate(0)(2)
        make_decay(1)
        make_p2(0)(2)
        make_rate(1)(2)
        make_p2(1)(2)
        make_a_sq(2)
        make_f_sq(4)
        make_x7(0)
        make_da(0)
        make_minus_f(4)
        make_x7(1)
        make_da(1)
        make_g_signed(2)
        flip_x7(0)
        flip_da(0)
        flip_m(0)
        flip_rate(2)
        for t in range(1, 4):
            make_bias_h(t)
        make_w1(0)
        regroup_da(0)
        make_df(0)
        make_u(2)
        flip_w_mod()
        for s in range(0, TILES + 4):
            if s == 2:
                copy_w_mod()
            if s == 3:
                weights = [quantise_weight(grouped_mod, "mod"), quantise_weight(grouped_tgt, "tgt")]
            step(s)
